import numpy as np
import ml_dtypes


def mxq(x, axis, fmt="e4m3"):
    dtype, down = {"e4m3": (ml_dtypes.float8_e4m3fn, 7), "e5m2": (ml_dtypes.float8_e5m2, 14)}[fmt]
    v = np.moveaxis(np.asarray(x, np.float32).astype(ml_dtypes.bfloat16).astype(np.float64), axis, -1)
    blocks = v.reshape(v.shape[:-1] + (-1, 32))
    amax = np.abs(blocks).max(-1, keepdims=True)
    byte = np.maximum(np.where(amax > 0, np.frexp(amax)[1] - 1 + 127, 0) - down, 1)
    scale = np.exp2(byte - 127.0)
    codes = (blocks / scale).astype(np.float32).astype(dtype).astype(np.float64)
    return np.moveaxis((codes * scale).reshape(v.shape), -1, axis)


WIDE = False


def mx_kscale(k):
    if not WIDE:
        return np.ones(k)
    levels = np.array([30, -30])
    if k % 512:
        return np.exp2(np.random.permutation(np.resize(levels, k // 32))).repeat(32)
    a = np.empty((k // 512, 16))
    for p in range(k // 512):
        a[p, :8] = np.random.permutation(np.resize(levels, 8))
        for g in range(8):
            far = levels[np.abs(levels - a[p, g]) >= 10]
            a[p, g + 8] = far[np.random.randint(len(far))]
    return np.exp2(a.ravel()).repeat(32)


BF16 = ml_dtypes.bfloat16


def bf(x):
    return np.asarray(x, np.float32).astype(BF16)


def f64(x):
    return np.asarray(x).astype(np.float64)


B, CIN, H, W, CP, G = 3, 2048, 16, 16, 1024, 2
CG = CP // G
CO = CIN // G
HW = H * W
EPS = 1e-5


def setup_inputs():
    s = mx_kscale(CG)
    return {"y": bf((np.random.standard_normal((B, G, CG, HW)) * 2.5 + 1.0) * s[None, None, :, None]),
            "Wz": bf((np.random.standard_normal((G, CO, CG)) / np.sqrt(CG) + 1.5 / CG) / s),
            "gamma": bf(1.0 + 0.1 * np.random.standard_normal(CIN)),
            "beta": bf(0.1 * np.random.standard_normal(CIN)),
            "x": bf(np.random.standard_normal((B, CIN, H, W)))}


def reference(y, Wz, gamma, beta, x):
    z = mxq(f64(Wz), 2, "e5m2") @ mxq(f64(y), 2, "e5m2")
    zr = z.reshape(B, G, CO * HW)
    mu = zr.mean(-1, keepdims=True)
    var = zr.var(-1, keepdims=True)
    zn = ((zr - mu) * (1.0 / np.sqrt(var + EPS))).reshape(B, CIN, H, W)
    return zn * f64(gamma)[None, :, None, None] + f64(beta)[None, :, None, None] + f64(x)

@@ -1,0 +1,391 @@
+from contextlib import ExitStack
+
+import concourse.mybir as mybir
+from concourse.masks import make_identity
+
+F32 = mybir.dt.float32
+BF16 = mybir.dt.bfloat16
+U32 = mybir.dt.uint32
+U8 = mybir.dt.uint8
+E5X4 = mybir.dt.float8_e5m2_x4
+ACT = mybir.ActivationFunctionType
+ALU = mybir.AluOpType
+AX = mybir.AxisListType
+
+B, G, CG, CO, HW = 3, 2, 512, 1024, 256
+P = 128
+T = CO // P
+EPS = 1e-5
+FLOPS = 2 * B * G * CO * CG * HW
+NV = 2
+
+
+def tile_spatialcgnl_pb_kernel(tc, y, Wz, gamma, beta, x, out):
+    nc = tc.nc
+    with ExitStack() as ctx:
+        keep = ctx.enter_context(tc.tile_pool(name="keep", bufs=1))
+        junkp = ctx.enter_context(tc.tile_pool(name="junkp", bufs=2))
+        psum_z = ctx.enter_context(tc.psum_pool(name="psum_z", bufs=6))
+        psum_a = ctx.enter_context(tc.psum_pool(name="psum_a", bufs=1))
+        psum_s = ctx.enter_context(tc.psum_pool(name="psum_s", bufs=1))
+
+        ident = keep.tile([P, P], F32, name="ident")
+        c_part = keep.tile([P, P], F32, name="c_part")
+        c_all = keep.tile([P, P], F32, name="c_all")
+        one = keep.tile([P, 1], F32, name="one")
+        warm = keep.tile([P, 1], F32, name="warm")
+        red = [keep.tile([P, B, 2, 4], F32, name="red%d" % j) for j in range(G)]
+        y_raw = [keep.tile([P, B, 4 * HW], BF16, name="y_raw%d" % j) for j in range(G)]
+        w_raw = [keep.tile([P, T, CG], BF16, name="w_raw%d" % j) for j in range(G)]
+        x_sb = [[keep.tile([P, T * HW], BF16, name="x_sb%d_%d" % (b, j)) for j in range(G)] for b in range(B)]
+        g_bf = keep.tile([P, G, T], BF16, name="g_bf")
+        b_bf = keep.tile([P, G, T], BF16, name="b_bf")
+        gam = keep.tile([P, G, T], F32, name="gam")
+        bet = keep.tile([P, G, T], F32, name="bet")
+        y_grp = [keep.tile([P, B, 4 * HW], BF16, name="y_grp%d" % j, align_bytes=64) for j in range(G)]
+        y_cod = [keep.tile([P, B * HW], U32, name="y_cod%d" % j, align_bytes=64) for j in range(G)]
+        y_scl = [keep.tile([P, B * HW], U8, name="y_scl%d" % j, align_bytes=64) for j in range(G)]
+        w_grp = [keep.tile([P, T * CG], BF16, name="w_grp%d" % j, align_bytes=64) for j in range(G)]
+        w_cod = [keep.tile([P, CO], U32, name="w_cod%d" % j, align_bytes=64) for j in range(G)]
+        w_scl = [keep.tile([P, CO], U8, name="w_scl%d" % j, align_bytes=64) for j in range(G)]
+        st = [keep.tile([P, NV, 4, 6], F32, name="st%d" % j) for j in range(G)]
+        a_sc = [keep.tile([P, B, T], F32, name="a_sc%d" % j) for j in range(G)]
+        b_sc = [keep.tile([P, B, T], F32, name="b_sc%d" % j) for j in range(G)]
+        xb = [[keep.tile([P, T * HW], F32, name="xb%d_%d" % (b, j)) for j in range(G)] for b in range(B)]
+        sq = [keep.tile([P, NV], F32, name="sq%d" % j) for j in range(G)]
+        tot = [keep.tile([P, B, 2], F32, name="tot%d" % j) for j in range(G)]
+        msq = [keep.tile([P, B], F32, name="msq%d" % j) for j in range(G)]
+        ve = [keep.tile([P, B], F32, name="ve%d" % j) for j in range(G)]
+        sd = [keep.tile([P, B], F32, name="sd%d" % j) for j in range(G)]
+        rstd = [keep.tile([P, B], F32, name="rstd%d" % j) for j in range(G)]
+        nmr = [keep.tile([P, B], F32, name="nmr%d" % j) for j in range(G)]
+        bank = {}
+
+        def y_view(j, b0, b1):
+            return y[b0:b1, j].rearrange("b (p q) w -> p b (q w)", q=4)
+
+        def w_view(j):
+            return Wz[j].rearrange("(p t) k -> p t k", t=T)
+
+        def chan_view(ap, b, j):
+            return ap[b].rearrange("(j p t) h w -> j p (t h w)", j=G, t=T)[j]
+
+        def load_y(j, b0, b1):
+            nc.sync.dma_start(out=y_raw[j][:, b0:b1, :], in_=y_view(j, b0, b1))
+
+        def load_w(j, t0, t1):
+            nc.sync.dma_start(out=w_raw[j][:, t0:t1, :], in_=w_view(j)[:, t0:t1, :])
+
+        def yi(j, b0, b1, eng):
+            if eng == "G":
+                for b in range(b0, b1):
+                    nc.gpsimd.tensor_scalar(
+                        out=y_grp[j][:, b, :].rearrange("p (w q) -> p w q", q=4),
+                        in0=y_raw[j][:, b, :].rearrange("p (q w) -> p w q", q=4),
+                        scalar1=1.0, scalar2=0.0, op0=ALU.mult, op1=ALU.add,
+                    )
+            else:
+                nc.vector.tensor_copy(
+                    out=y_grp[j][:, b0:b1, :].rearrange("p b (w q) -> p b w q", q=4),
+                    in_=y_raw[j][:, b0:b1, :].rearrange("p b (q w) -> p b w q", q=4),
+                )
+
+        def yq(j, b0, b1):
+            nc.vector.quantize_mx(
+                out=y_cod[j][:, b0 * HW:b1 * HW].bitcast(E5X4),
+                scales=y_scl[j][:, b0 * HW:b1 * HW],
+                in_=y_grp[j][:, b0:b1, :].rearrange("p b c -> p (b c)"),
+            )
+
+        def tr(j, s):
+            words = w_raw[j][:].bitcast(F32)
+            z = psum_z.tile([P, 512], F32, name="z")
+            bank[("t", j, s)] = z
+            tp = z[:].rearrange("p (s u r) -> p s u r", s=2, u=2)
+            for tt in range(2):
+                for u in range(2):
+                    nc.tensor.transpose(tp[:, tt, u, :], words[:, 2 * s + tt, u:CG // 2:2], ident[:])
+
+        def wc(j, s):
+            gwords = w_grp[j][:].bitcast(F32)
+            nc.scalar.copy(
+                out=gwords[:, 512 * s:512 * (s + 1)].rearrange("p (s r u) -> p s r u", s=2, u=2),
+                in_=bank[("t", j, s)][:].rearrange("p (s u r) -> p s r u", s=2, u=2),
+            )
+
+        def wq(j, s):
+            nc.vector.quantize_mx(
+                out=w_cod[j][:, 256 * s:256 * (s + 1)].bitcast(E5X4),
+                scales=w_scl[j][:, 256 * s:256 * (s + 1)],
+                in_=w_grp[j][:, 1024 * s:1024 * (s + 1)],
+            )
+
+        def mm_stat(z, j, b, m, h, start, stop):
+            c0 = b * HW + P * m
+            nc.tensor.matmul_mx(
+                out=z[:],
+                lhsT=y_cod[j][:, c0:c0 + P].bitcast(E5X4),
+                lhsT_scale=y_scl[j][:, c0:c0 + P],
+                rhs=w_cod[j][:, 512 * h:512 * (h + 1)].bitcast(E5X4),
+                rhs_scale=w_scl[j][:, 512 * h:512 * (h + 1)],
+                start=start,
+                stop=stop,
+            )
+
+        def ms(j, h, b, m):
+            z = psum_z.tile([P, 512], F32, name="z")
+            bank[("s", j, h, b, m)] = z
+            mm_stat(z, j, b, m, h, True, True)
+            if b >= NV:
+                if (h, m) == (0, 0):
+                    bank[("a", j, b)] = psum_a.tile([P, 512], F32, name="za")
+                mm_stat(bank[("a", j, b)], j, b, m, h, (h, m) == (0, 0), (h, m) == (1, 1))
+
+        def us(j, h, b, m):
+            z = bank[("s", j, h, b, m)]
+            if b < NV:
+                nc.vector.bn_stats(out=st[j][:, b, 2 * h + m, :], in_=z[:])
+            else:
+                jk = junkp.tile([P, 512], BF16, name="jk")
+                nc.scalar.activation(out=jk[:], in_=z[:], func=ACT.Square,
+                                     accum_out=red[j][:, b, 1, 2 * h + m:2 * h + m + 1])
+                if (h, m) == (1, 1):
+                    jk = junkp.tile([P, 512], BF16, name="jk")
+                    nc.scalar.activation(out=jk[:], in_=bank[("a", j, b)][:], func=ACT.Identity,
+                                         accum_out=red[j][:, b, 0, 0:1])
+
+        def stat(j, h, b, m):
+            ms(j, h, b, m)
+            us(j, h, b, m)
+
+        def c1(j):
+            for i in range(NV):
+                nc.vector.bn_aggr(out=red[j][:, i, :, 0], in_=st[j][:, i, :, :].rearrange("p c s -> p (c s)"))
+            nc.vector.tensor_tensor(out=sq[j][:], in0=red[j][:, 0:NV, 0, 0], in1=red[j][:, 0:NV, 0, 0], op=ALU.mult)
+            nc.vector.tensor_tensor(out=red[j][:, 0:NV, 1, 0], in0=red[j][:, 0:NV, 1, 0], in1=sq[j][:], op=ALU.add)
+
+        def cm(j):
+            ps = psum_s.tile([P, B, 2, 4], F32, name="ps")
+            bank[("c", j)] = ps
+            nc.tensor.matmul(ps[:, 0:NV].rearrange("p i k f -> p (i k f)"), lhsT=c_part[:],
+                             rhs=red[j][:, 0:NV].rearrange("p i k f -> p (i k f)"), start=True, stop=True)
+            nc.tensor.matmul(ps[:, NV:B].rearrange("p i k f -> p (i k f)"), lhsT=c_all[:],
+                             rhs=red[j][:, NV:B].rearrange("p i k f -> p (i k f)"), start=True, stop=True)
+
+        def c2(j):
+            nc.vector.tensor_reduce(out=tot[j][:].rearrange("p i k -> p (i k)"),
+                                    in_=bank[("c", j)][:].rearrange("p i k f -> p (i k) f"), axis=AX.X, op=ALU.add)
+            nc.vector.tensor_tensor(out=msq[j][:], in0=tot[j][:, :, 0], in1=tot[j][:, :, 0], op=ALU.mult)
+            nc.vector.scalar_tensor_tensor(out=ve[j][:], in0=tot[j][:, :, 1], scalar=EPS, in1=msq[j][:],
+                                           op0=ALU.add, op1=ALU.subtract)
+
+        def cs(j):
+            nc.scalar.activation(out=sd[j][:], in_=ve[j][:], func=ACT.Sqrt)
+
+        def c3(j):
+            nc.vector.reciprocal(out=rstd[j][:], in_=sd[j][:])
+            nc.vector.scalar_tensor_tensor(out=nmr[j][:], in0=tot[j][:, :, 0], scalar=-1.0, in1=rstd[j][:],
+                                           op0=ALU.mult, op1=ALU.mult)
+            gam_b = gam[:, j:j + 1, :].to_broadcast([P, B, T])
+            bet_b = bet[:, j:j + 1, :].to_broadcast([P, B, T])
+            nc.vector.tensor_tensor(out=a_sc[j][:], in0=gam_b, in1=rstd[j][:].unsqueeze(2).to_broadcast([P, B, T]),
+                                    op=ALU.mult)
+            nc.vector.tensor_tensor(out=b_sc[j][:], in0=gam_b, in1=nmr[j][:].unsqueeze(2).to_broadcast([P, B, T]),
+                                    op=ALU.mult)
+            nc.vector.tensor_tensor(out=b_sc[j][:], in0=b_sc[j][:], in1=bet_b, op=ALU.add)
+
+        def cols(t0, t1):
+            return slice(t0 * HW, t1 * HW)
+
+        def xp(j, b, t, eng):
+            if eng == "G":
+                nc.gpsimd.tensor_scalar(out=xb[b][j][:, cols(t, t + 1)], in0=x_sb[b][j][:, cols(t, t + 1)],
+                                        scalar1=one[:, 0:1], scalar2=b_sc[j][:, b, t:t + 1],
+                                        op0=ALU.mult, op1=ALU.add)
+            else:
+                nc.scalar.activation(out=xb[b][j][:, cols(t, t + 1)], in_=x_sb[b][j][:, cols(t, t + 1)],
+                                     func=ACT.Identity, bias=b_sc[j][:, b, t:t + 1], scale=1.0)
+
+        def mm_apply(j, t, c0):
+            z = psum_z.tile([P, 512], F32, name="z")
+            nc.tensor.matmul_mx(
+                out=z[:],
+                lhsT=w_cod[j][:, P * t:P * (t + 1)].bitcast(E5X4),
+                lhsT_scale=w_scl[j][:, P * t:P * (t + 1)],
+                rhs=y_cod[j][:, c0:c0 + 512].bitcast(E5X4),
+                rhs_scale=y_scl[j][:, c0:c0 + 512],
+                start=True,
+                stop=True,
+            )
+            return z
+
+        def ma(j, t):
+            bank[("A", j, t)] = mm_apply(j, t, 0)
+
+        def mb(j, t):
+            bank[("B", j, t)] = mm_apply(j, t, HW)
+
+        def zhalf(j, b, t):
+            if b < 2:
+                return bank[("A", j, t)][:, b * HW:(b + 1) * HW]
+            return bank[("B", j, t)][:, HW:2 * HW]
+
+        def stt(j, b, t):
+            nc.vector.scalar_tensor_tensor(out=xb[b][j][:, cols(t, t + 1)], in0=zhalf(j, b, t),
+                                           scalar=a_sc[j][:, b, t:t + 1], in1=xb[b][j][:, cols(t, t + 1)],
+                                           op0=ALU.mult, op1=ALU.add)
+
+        def af(j, b, t):
+            nc.scalar.activation(out=xb[b][j][:, cols(t, t + 1)], in_=zhalf(j, b, t), func=ACT.Identity,
+                                 bias=b_sc[j][:, b, t:t + 1], scale=a_sc[j][:, b, t:t + 1])
+
+        def ga(j, b, t0, t1):
+            nc.gpsimd.tensor_tensor(out=xb[b][j][:, cols(t0, t1)], in0=xb[b][j][:, cols(t0, t1)],
+                                    in1=x_sb[b][j][:, cols(t0, t1)], op=ALU.add)
+
+        def so(j, b, t0, t1):
+            nc.sync.dma_start(out=chan_view(out, b, j)[:, cols(t0, t1)], in_=xb[b][j][:, cols(t0, t1)])
+
+        make_identity(nc, ident[:])
+        nc.gpsimd.memset(c_part[:], 1.0 / P)
+        nc.gpsimd.memset(c_all[:], 1.0 / (CO * HW))
+        nc.vector.memset(one[:], 1.0)
+        nc.scalar.activation(out=warm[:], in_=one[:], func=ACT.Sqrt)
+        for j in range(G):
+            nc.gpsimd.memset(red[j][:], 0.0)
+
+        ctx.enter_context(tc.manual_schedule())
+
+        load_y(0, 0, 1)
+        load_y(0, 1, 2)
+        load_w(0, 0, 2)
+        load_w(0, 2, 4)
+        load_y(0, 2, 3)
+        load_w(0, 4, 6)
+        load_w(0, 6, 8)
+        nc.sync.dma_start(out=g_bf[:], in_=gamma.rearrange("(j p t) -> p j t", j=G, t=T))
+        nc.sync.dma_start(out=b_bf[:], in_=beta.rearrange("(j p t) -> p j t", j=G, t=T))
+        load_y(1, 0, 3)
+        load_w(1, 0, 4)
+        load_w(1, 4, 8)
+        for j in range(G):
+            for b in range(B):
+                nc.sync.dma_start(out=x_sb[b][j][:], in_=chan_view(x, b, j))
+
+        yi(0, 0, 1, "V")
+        yi(0, 1, 2, "V")
+        yq(0, 0, 2)
+        for s in range(4):
+            tr(0, s)
+        for s in range(4):
+            wc(0, s)
+        yi(0, 2, 3, "V")
+        yq(0, 2, 3)
+        wq(0, 0)
+        wq(0, 1)
+        yi(1, 0, 3, "G")
+        nc.gpsimd.tensor_copy(out=gam[:], in_=g_bf[:])
+        nc.gpsimd.tensor_copy(out=bet[:], in_=b_bf[:])
+
+        stat(0, 0, 0, 0)
+        stat(0, 0, 2, 0)
+        wq(0, 2)
+        stat(0, 0, 0, 1)
+        wq(0, 3)
+        stat(0, 0, 1, 0)
+        stat(0, 0, 2, 1)
+        stat(0, 0, 1, 1)
+        for (b, m) in ((0, 0), (2, 0), (0, 1), (1, 0), (2, 1), (1, 1)):
+            stat(0, 1, b, m)
+
+        tr(1, 0)
+        tr(1, 1)
+        c1(0)
+        cm(0)
+        tr(1, 2)
+        tr(1, 3)
+        wc(1, 0)
+        wc(1, 1)
+        yq(1, 0, 2)
+        c2(0)
+        cs(0)
+        wc(1, 2)
+        wc(1, 3)
+        yq(1, 2, 3)
+        wq(1, 0)
+        c3(0)
+        wq(1, 1)
+        wq(1, 2)
+        wq(1, 3)
+
+        def xp0(t):
+            xp(0, 0, t, "S")
+            xp(0, 1, t, "S")
+
+        def st0(t):
+            stt(0, 0, t)
+            stt(0, 1, t)
+
+        VB = ((0, 0), (0, 1), (1, 0), (1, 1))
+        xp0(0)
+        xp0(1)
+        for i in range(4):
+            (b, m) = VB[i]
+            ms(1, 0, b, m)
+            mb(0, i)
+            us(1, 0, b, m)
+            af(0, 2, i)
+        ga(0, 2, 0, 4)
+        xp0(2)
+        xp0(3)
+        for i in range(4):
+            ma(0, i)
+            mb(0, 4 + i)
+            st0(i)
+            af(0, 2, 4 + i)
+        ga(0, 2, 4, 8)
+        for b in range(B):
+            so(0, b, 0, 4)
+        stat(1, 1, 0, 0)
+        stat(1, 0, 2, 0)
+        stat(1, 1, 0, 1)
+        stat(1, 0, 2, 1)
+        xp0(4)
+        xp0(5)
+        stat(1, 1, 1, 0)
+        stat(1, 1, 2, 0)
+        stat(1, 1, 1, 1)
+        ma(0, 4)
+        stat(1, 1, 2, 1)
+        so(0, 2, 4, 8)
+        ma(0, 5)
+        ma(0, 6)
+        st0(4)
+        st0(5)
+        xp0(6)
+        xp0(7)
+        c1(1)
+        cm(1)
+        ma(0, 7)
+        st0(6)
+        c2(1)
+        cs(1)
+        st0(7)
+        c3(1)
+        for b in range(2):
+            so(0, b, 4, 8)
+
+        for t in range(T):
+            xp(1, 0, t, "S")
+            xp(1, 1, t, "S")
+            xp(1, 2, t, "G")
+        STORES = ((0, 2), (2, 4), (4, 6), (6, 7), (7, 8))
+        for t in range(T):
+            ma(1, t)
+            mb(1, t)
+            for b in range(B):
+                stt(1, b, t)
+            for (t0, t1) in STORES:
+                if t == t1 - 1:
+                    for b in range(B):
+                        so(1, b, t0, t1)

@@ -17,6 +17,7 @@ P = 128
 T = CO // P
 EPS = 1e-5
 FLOPS = 2 * B * G * CO * CG * HW
+NWARM = 9
 NV = 2
 
 
@@ -42,13 +43,15 @@ def tile_spatialcgnl_pb_kernel(tc, y, Wz, gamma, beta, x, out):
         b_bf = keep.tile([P, G, T], BF16, name="b_bf")
         gam = keep.tile([P, G, T], F32, name="gam")
         bet = keep.tile([P, G, T], F32, name="bet")
-        y_grp = [keep.tile([P, B, 4 * HW], BF16, name="y_grp%d" % j, align_bytes=64) for j in range(G)]
+        y_grp = [keep.tile([P, B, 4 * HW], BF16, name="y_grp0", align_bytes=64), None]
         y_cod = [keep.tile([P, B * HW], U32, name="y_cod%d" % j, align_bytes=64) for j in range(G)]
         y_scl = [keep.tile([P, B * HW], U8, name="y_scl%d" % j, align_bytes=64) for j in range(G)]
-        w_grp = [keep.tile([P, T * CG], BF16, name="w_grp%d" % j, align_bytes=64) for j in range(G)]
+        w_grp = [keep.tile([P, T * CG], BF16, name="w_grp0", tag="shared", align_bytes=64),
+                 keep.tile([P, T * CG], BF16, name="w_grp1", align_bytes=64)]
+        wz = keep.tile([P, 512], BF16, name="wz")
         w_cod = [keep.tile([P, CO], U32, name="w_cod%d" % j, align_bytes=64) for j in range(G)]
         w_scl = [keep.tile([P, CO], U8, name="w_scl%d" % j, align_bytes=64) for j in range(G)]
-        st = [keep.tile([P, NV, 4, 6], F32, name="st%d" % j) for j in range(G)]
+        st = [keep.tile([P, T, 6], F32, name="st%d" % j) for j in range(G)]
         a_sc = [keep.tile([P, B, T], F32, name="a_sc%d" % j) for j in range(G)]
         b_sc = [keep.tile([P, B, T], F32, name="b_sc%d" % j) for j in range(G)]
         xb = [[keep.tile([P, T * HW], F32, name="xb%d_%d" % (b, j)) for j in range(G)] for b in range(B)]
@@ -158,11 +161,19 @@ def tile_spatialcgnl_pb_kernel(tc, y, Wz, gamma, beta, x, out):
             ms(j, h, b, m)
             us(j, h, b, m)
 
-        def c1(j):
-            for i in range(NV):
-                nc.vector.bn_aggr(out=red[j][:, i, :, 0], in_=st[j][:, i, :, :].rearrange("p c s -> p (c s)"))
-            nc.vector.tensor_tensor(out=sq[j][:], in0=red[j][:, 0:NV, 0, 0], in1=red[j][:, 0:NV, 0, 0], op=ALU.mult)
-            nc.vector.tensor_tensor(out=red[j][:, 0:NV, 1, 0], in0=red[j][:, 0:NV, 1, 0], in1=sq[j][:], op=ALU.add)
+        def mx(j, t):
+            bank[("X", j, t)] = mm_apply(j, t, 0)
+
+        def bna(j, t):
+            nc.vector.bn_stats(out=st[j][:, t, :], in_=bank[("X", j, t)][:].rearrange("p (i n) -> p n i", i=2))
+
+        def ag(j, i):
+            nc.vector.bn_aggr(out=red[j][:, i, :, 0], in_=st[j][:, :, 3 * i:3 * i + 3])
+
+        def e2(j, i):
+            nc.vector.scalar_tensor_tensor(out=red[j][:, i, 1, 0:1], in0=red[j][:, i, 0, 0:1],
+                                           scalar=red[j][:, i, 0, 0:1], in1=red[j][:, i, 1, 0:1],
+                                           op0=ALU.mult, op1=ALU.add)
 
         def cm(j):
             ps = psum_s.tile([P, B, 2, 4], F32, name="ps")
@@ -172,27 +183,35 @@ def tile_spatialcgnl_pb_kernel(tc, y, Wz, gamma, beta, x, out):
             nc.tensor.matmul(ps[:, NV:B].rearrange("p i k f -> p (i k f)"), lhsT=c_all[:],
                              rhs=red[j][:, NV:B].rearrange("p i k f -> p (i k f)"), start=True, stop=True)
 
-        def c2(j):
-            nc.vector.tensor_reduce(out=tot[j][:].rearrange("p i k -> p (i k)"),
-                                    in_=bank[("c", j)][:].rearrange("p i k f -> p (i k) f"), axis=AX.X, op=ALU.add)
-            nc.vector.tensor_tensor(out=msq[j][:], in0=tot[j][:, :, 0], in1=tot[j][:, :, 0], op=ALU.mult)
-            nc.vector.scalar_tensor_tensor(out=ve[j][:], in0=tot[j][:, :, 1], scalar=EPS, in1=msq[j][:],
-                                           op0=ALU.add, op1=ALU.subtract)
+        def c2(j, k):
+            if k == 0:
+                nc.vector.tensor_reduce(out=tot[j][:].rearrange("p i k -> p (i k)"),
+                                        in_=bank[("c", j)][:].rearrange("p i k f -> p (i k) f"), axis=AX.X, op=ALU.add)
+            elif k == 1:
+                nc.vector.tensor_tensor(out=msq[j][:], in0=tot[j][:, :, 0], in1=tot[j][:, :, 0], op=ALU.mult)
+            else:
+                nc.vector.scalar_tensor_tensor(out=ve[j][:], in0=tot[j][:, :, 1], scalar=EPS, in1=msq[j][:],
+                                               op0=ALU.add, op1=ALU.subtract)
 
         def cs(j):
             nc.scalar.activation(out=sd[j][:], in_=ve[j][:], func=ACT.Sqrt)
 
-        def c3(j):
-            nc.vector.reciprocal(out=rstd[j][:], in_=sd[j][:])
-            nc.vector.scalar_tensor_tensor(out=nmr[j][:], in0=tot[j][:, :, 0], scalar=-1.0, in1=rstd[j][:],
-                                           op0=ALU.mult, op1=ALU.mult)
+        def c3(j, k):
             gam_b = gam[:, j:j + 1, :].to_broadcast([P, B, T])
             bet_b = bet[:, j:j + 1, :].to_broadcast([P, B, T])
-            nc.vector.tensor_tensor(out=a_sc[j][:], in0=gam_b, in1=rstd[j][:].unsqueeze(2).to_broadcast([P, B, T]),
-                                    op=ALU.mult)
-            nc.vector.tensor_tensor(out=b_sc[j][:], in0=gam_b, in1=nmr[j][:].unsqueeze(2).to_broadcast([P, B, T]),
-                                    op=ALU.mult)
-            nc.vector.tensor_tensor(out=b_sc[j][:], in0=b_sc[j][:], in1=bet_b, op=ALU.add)
+            if k == 0:
+                nc.vector.reciprocal(out=rstd[j][:], in_=sd[j][:])
+            elif k == 1:
+                nc.vector.scalar_tensor_tensor(out=nmr[j][:], in0=tot[j][:, :, 0], scalar=-1.0, in1=rstd[j][:],
+                                               op0=ALU.mult, op1=ALU.mult)
+            elif k == 2:
+                nc.vector.tensor_tensor(out=a_sc[j][:], in0=gam_b,
+                                        in1=rstd[j][:].unsqueeze(2).to_broadcast([P, B, T]), op=ALU.mult)
+            elif k == 3:
+                nc.vector.tensor_tensor(out=b_sc[j][:], in0=gam_b,
+                                        in1=nmr[j][:].unsqueeze(2).to_broadcast([P, B, T]), op=ALU.mult)
+            else:
+                nc.vector.tensor_tensor(out=b_sc[j][:], in0=b_sc[j][:], in1=bet_b, op=ALU.add)
 
         def cols(t0, t1):
             return slice(t0 * HW, t1 * HW)
@@ -247,6 +266,7 @@ def tile_spatialcgnl_pb_kernel(tc, y, Wz, gamma, beta, x, out):
             nc.sync.dma_start(out=chan_view(out, b, j)[:, cols(t0, t1)], in_=xb[b][j][:, cols(t0, t1)])
 
         make_identity(nc, ident[:])
+        nc.vector.memset(wz[:], 0.0)
         nc.gpsimd.memset(c_part[:], 1.0 / P)
         nc.gpsimd.memset(c_all[:], 1.0 / (CO * HW))
         nc.vector.memset(one[:], 1.0)
@@ -259,126 +279,155 @@ def tile_spatialcgnl_pb_kernel(tc, y, Wz, gamma, beta, x, out):
         load_y(0, 0, 1)
         load_y(0, 1, 2)
         load_w(0, 0, 2)
-        load_w(0, 2, 4)
         load_y(0, 2, 3)
+        load_w(0, 2, 4)
         load_w(0, 4, 6)
         load_w(0, 6, 8)
-        nc.sync.dma_start(out=g_bf[:], in_=gamma.rearrange("(j p t) -> p j t", j=G, t=T))
-        nc.sync.dma_start(out=b_bf[:], in_=beta.rearrange("(j p t) -> p j t", j=G, t=T))
         load_y(1, 0, 3)
         load_w(1, 0, 4)
         load_w(1, 4, 8)
+        nc.sync.dma_start(out=g_bf[:], in_=gamma.rearrange("(j p t) -> p j t", j=G, t=T))
+        nc.sync.dma_start(out=b_bf[:], in_=beta.rearrange("(j p t) -> p j t", j=G, t=T))
         for j in range(G):
             for b in range(B):
                 nc.sync.dma_start(out=x_sb[b][j][:], in_=chan_view(x, b, j))
 
+        pw = psum_s.tile([P, 512], F32, name="ps")
+        for i in range(NWARM):
+            nc.tensor.matmul(pw[:], lhsT=wz[:, 0:P], rhs=wz[:], start=True, stop=True)
+
+        def stat_a(j, t):
+            mx(j, t)
+            bna(j, t)
+
+        def stat_s(j, h, m):
+            ms(j, h, 2, m)
+            us(j, h, 2, m)
+
         yi(0, 0, 1, "V")
         yi(0, 1, 2, "V")
         yq(0, 0, 2)
-        for s in range(4):
-            tr(0, s)
-        for s in range(4):
-            wc(0, s)
+        tr(0, 0)
+        wc(0, 0)
+        tr(0, 1)
+        wc(0, 1)
+        wq(0, 0)
         yi(0, 2, 3, "V")
         yq(0, 2, 3)
-        wq(0, 0)
         wq(0, 1)
-        yi(1, 0, 3, "G")
+        mx(0, 0)
+        mx(0, 1)
+        tr(0, 2)
+        wc(0, 2)
+        mx(0, 2)
+        mx(0, 3)
+        tr(0, 3)
+        wc(0, 3)
+        bna(0, 0)
+        bna(0, 1)
+        wq(0, 2)
+        bna(0, 2)
+        bna(0, 3)
+        wq(0, 3)
+        y_grp[1] = keep.tile([P, B, 4 * HW], BF16, name="y_grp1", tag="shared", align_bytes=64)
+        yi(1, 0, 2, "G")
         nc.gpsimd.tensor_copy(out=gam[:], in_=g_bf[:])
         nc.gpsimd.tensor_copy(out=bet[:], in_=b_bf[:])
+        stat_s(0, 0, 0)
+        stat_a(0, 4)
+        stat_s(0, 0, 1)
+        stat_a(0, 5)
+        stat_s(0, 1, 0)
+        stat_a(0, 6)
+        stat_s(0, 1, 1)
+        stat_a(0, 7)
 
-        stat(0, 0, 0, 0)
-        stat(0, 0, 2, 0)
-        wq(0, 2)
-        stat(0, 0, 0, 1)
-        wq(0, 3)
-        stat(0, 0, 1, 0)
-        stat(0, 0, 2, 1)
-        stat(0, 0, 1, 1)
-        for (b, m) in ((0, 0), (2, 0), (0, 1), (1, 0), (2, 1), (1, 1)):
-            stat(0, 1, b, m)
-
-        tr(1, 0)
-        tr(1, 1)
-        c1(0)
-        cm(0)
-        tr(1, 2)
-        tr(1, 3)
-        wc(1, 0)
-        wc(1, 1)
-        yq(1, 0, 2)
-        c2(0)
-        cs(0)
-        wc(1, 2)
-        wc(1, 3)
+        for s in range(4):
+            tr(1, s)
+        for s in range(4):
+            wc(1, s)
+        yi(1, 2, 3, "V")
+        ag(0, 0)
+        ag(0, 1)
         yq(1, 2, 3)
+        e2(0, 0)
+        e2(0, 1)
+        cm(0)
+        yq(1, 0, 2)
         wq(1, 0)
-        c3(0)
         wq(1, 1)
+        c2(0, 0)
         wq(1, 2)
+        c2(0, 1)
         wq(1, 3)
+        c2(0, 2)
+        cs(0)
 
-        def xp0(t):
-            xp(0, 0, t, "S")
-            xp(0, 1, t, "S")
+        xq = [(b, t) for t in range(T) for b in range(B)]
 
-        def st0(t):
-            stt(0, 0, t)
-            stt(0, 1, t)
+        xn = [0]
 
-        VB = ((0, 0), (0, 1), (1, 0), (1, 1))
-        xp0(0)
-        xp0(1)
-        for i in range(4):
-            (b, m) = VB[i]
-            ms(1, 0, b, m)
-            mb(0, i)
-            us(1, 0, b, m)
-            af(0, 2, i)
-        ga(0, 2, 0, 4)
-        xp0(2)
-        xp0(3)
-        for i in range(4):
-            ma(0, i)
-            mb(0, 4 + i)
-            st0(i)
-            af(0, 2, 4 + i)
-        ga(0, 2, 4, 8)
-        for b in range(B):
-            so(0, b, 0, 4)
-        stat(1, 1, 0, 0)
-        stat(1, 0, 2, 0)
-        stat(1, 1, 0, 1)
-        stat(1, 0, 2, 1)
-        xp0(4)
-        xp0(5)
-        stat(1, 1, 1, 0)
-        stat(1, 1, 2, 0)
-        stat(1, 1, 1, 1)
-        ma(0, 4)
-        stat(1, 1, 2, 1)
-        so(0, 2, 4, 8)
-        ma(0, 5)
-        ma(0, 6)
-        st0(4)
-        st0(5)
-        xp0(6)
-        xp0(7)
-        c1(1)
-        cm(1)
-        ma(0, 7)
-        st0(6)
-        c2(1)
-        cs(1)
-        st0(7)
-        c3(1)
-        for b in range(2):
-            so(0, b, 4, 8)
+        def xpush(n):
+            for i in range(n):
+                if xn[0] < len(xq):
+                    (b, t) = xq[xn[0]]
+                    xn[0] += 1
+                    xp(0, b, t, "S")
+
+        SB = ((0, 0), (0, 1), (1, 0), (1, 1))
+        C3 = ((), (0,), (1, 2), (3,), (4,), (), (), ())
+        for t in range(T):
+            stat_a(1, t)
+            for k in C3[t]:
+                c3(0, k)
+            if t % 2 == 1:
+                (h, m) = SB[t // 2]
+                stat_s(1, h, m)
+                if t >= 5:
+                    xpush(3)
+
+        CH = (("ag",), ("e2",), (), (), (), ("c2", 0), ("c2", 1), ("c2", 2), (), (), ("c3", 0), ("c3", 1, 2), ("c3", 3), ("c3", 4))
+        issued = [0]
+
+        def m_issue(n):
+            while issued[0] < min(n, T):
+                ma(0, issued[0])
+                mb(0, issued[0])
+                issued[0] += 1
+
+        m_issue(2)
+        hi = 0
+        for t in range(T):
+            for b in range(B):
+                if hi < len(CH):
+                    step = CH[hi]
+                    hi += 1
+                    if step and step[0] == "ag":
+                        ag(1, 0)
+                        ag(1, 1)
+                    elif step and step[0] == "e2":
+                        e2(1, 0)
+                        e2(1, 1)
+                        cm(1)
+                    elif step and step[0] == "c2":
+                        c2(1, step[1])
+                        if step[1] == 2:
+                            cs(1)
+                    elif step and step[0] == "c3":
+                        for k in step[1:]:
+                            c3(1, k)
+                stt(0, b, t)
+                if hi == 2:
+                    m_issue(3)
+            m_issue(t + 3)
+            xpush(3)
+            if t % 2 == 1:
+                for b in range(B):
+                    so(0, b, t - 1, t + 1)
 
         for t in range(T):
-            xp(1, 0, t, "S")
-            xp(1, 1, t, "S")
-            xp(1, 2, t, "G")
+            for b in range(B):
+                xp(1, b, t, "S")
         STORES = ((0, 2), (2, 4), (4, 6), (6, 7), (7, 8))
         for t in range(T):
             ma(1, t)

@@ -17,7 +17,7 @@ P = 128
 T = CO // P
 EPS = 1e-5
 FLOPS = 2 * B * G * CO * CG * HW
-NWARM = 9
+NWARM = 0
 NV = 2
 
 
@@ -266,7 +266,6 @@ def tile_spatialcgnl_pb_kernel(tc, y, Wz, gamma, beta, x, out):
             nc.sync.dma_start(out=chan_view(out, b, j)[:, cols(t0, t1)], in_=xb[b][j][:, cols(t0, t1)])
 
         make_identity(nc, ident[:])
-        nc.vector.memset(wz[:], 0.0)
         nc.gpsimd.memset(c_part[:], 1.0 / P)
         nc.gpsimd.memset(c_all[:], 1.0 / (CO * HW))
         nc.vector.memset(one[:], 1.0)
@@ -292,9 +291,6 @@ def tile_spatialcgnl_pb_kernel(tc, y, Wz, gamma, beta, x, out):
             for b in range(B):
                 nc.sync.dma_start(out=x_sb[b][j][:], in_=chan_view(x, b, j))
 
-        pw = psum_s.tile([P, 512], F32, name="ps")
-        for i in range(NWARM):
-            nc.tensor.matmul(pw[:], lhsT=wz[:, 0:P], rhs=wz[:], start=True, stop=True)
 
         def stat_a(j, t):
             mx(j, t)

@@ -21,6 +21,10 @@ NWARM = 0
 NV = 2
 
 
+def a2(t):
+    return t % 2 == 0
+
+
 def tile_spatialcgnl_pb_kernel(tc, y, Wz, gamma, beta, x, out):
     nc = tc.nc
     with ExitStack() as ctx:
@@ -359,7 +363,7 @@ def tile_spatialcgnl_pb_kernel(tc, y, Wz, gamma, beta, x, out):
         c2(0, 2)
         cs(0)
 
-        xq = [(b, t) for t in range(T) for b in range(B)]
+        xq = [(b, t) for t in range(T) for b in range(2)]
 
         xn = [0]
 
@@ -376,11 +380,15 @@ def tile_spatialcgnl_pb_kernel(tc, y, Wz, gamma, beta, x, out):
             stat_a(1, t)
             for k in C3[t]:
                 c3(0, k)
+                if k == 4:
+                    for tt in range(T):
+                        if not a2(tt):
+                            xp(0, 2, tt, "G")
             if t % 2 == 1:
                 (h, m) = SB[t // 2]
                 stat_s(1, h, m)
                 if t >= 5:
-                    xpush(3)
+                    xpush(2)
 
         CH = (("ag",), ("e2",), (), (), (), ("c2", 0), ("c2", 1), ("c2", 2), (), (), ("c3", 0), ("c3", 1, 2), ("c3", 3), ("c3", 4))
         issued = [0]
@@ -394,7 +402,10 @@ def tile_spatialcgnl_pb_kernel(tc, y, Wz, gamma, beta, x, out):
         m_issue(2)
         hi = 0
         for t in range(T):
-            for b in range(B):
+            if a2(t):
+                af(0, 2, t)
+                ga(0, 2, t, t + 1)
+            for b in range(2 if a2(t) else B):
                 if hi < len(CH):
                     step = CH[hi]
                     hi += 1
@@ -416,19 +427,31 @@ def tile_spatialcgnl_pb_kernel(tc, y, Wz, gamma, beta, x, out):
                 if hi == 2:
                     m_issue(3)
             m_issue(t + 3)
-            xpush(3)
+            xpush(2)
             if t % 2 == 1:
                 for b in range(B):
                     so(0, b, t - 1, t + 1)
 
         for t in range(T):
-            for b in range(B):
-                xp(1, b, t, "S")
+            if not a2(t):
+                xp(1, 2, t, "G")
+
+        def xrow1(t):
+            xp(1, 0, t, "S")
+            xp(1, 1, t, "S")
+
+        xrow1(0)
+        xrow1(1)
         STORES = ((0, 2), (2, 4), (4, 6), (6, 7), (7, 8))
         for t in range(T):
             ma(1, t)
             mb(1, t)
-            for b in range(B):
+            if a2(t):
+                af(1, 2, t)
+                ga(1, 2, t, t + 1)
+            if t + 2 < T:
+                xrow1(t + 2)
+            for b in range(2 if a2(t) else B):
                 stt(1, b, t)
             for (t0, t1) in STORES:
                 if t == t1 - 1:

@@ -17,8 +17,13 @@ P = 128
 T = CO // P
 EPS = 1e-5
 FLOPS = 2 * B * G * CO * CG * HW
+NBN = 6 * T
+NST = NBN + 8
 NWARM = 0
 NV = 2
+
+
+XP0 = 3
 
 
 def a2(t):
@@ -35,11 +40,9 @@ def tile_spatialcgnl_pb_kernel(tc, y, Wz, gamma, beta, x, out):
         psum_s = ctx.enter_context(tc.psum_pool(name="psum_s", bufs=1))
 
         ident = keep.tile([P, P], F32, name="ident")
-        c_part = keep.tile([P, P], F32, name="c_part")
         c_all = keep.tile([P, P], F32, name="c_all")
         one = keep.tile([P, 1], F32, name="one")
         warm = keep.tile([P, 1], F32, name="warm")
-        red = [keep.tile([P, B, 2, 4], F32, name="red%d" % j) for j in range(G)]
         y_raw = [keep.tile([P, B, 4 * HW], BF16, name="y_raw%d" % j) for j in range(G)]
         w_raw = [keep.tile([P, T, CG], BF16, name="w_raw%d" % j) for j in range(G)]
         x_sb = [[keep.tile([P, T * HW], BF16, name="x_sb%d_%d" % (b, j)) for j in range(G)] for b in range(B)]
@@ -55,17 +58,16 @@ def tile_spatialcgnl_pb_kernel(tc, y, Wz, gamma, beta, x, out):
         wz = keep.tile([P, 512], BF16, name="wz")
         w_cod = [keep.tile([P, CO], U32, name="w_cod%d" % j, align_bytes=64) for j in range(G)]
         w_scl = [keep.tile([P, CO], U8, name="w_scl%d" % j, align_bytes=64) for j in range(G)]
-        st = [keep.tile([P, T, 6], F32, name="st%d" % j) for j in range(G)]
+        st = [keep.tile([P, NST], F32, name="st%d" % j) for j in range(G)]
+        gmn = [keep.tile([P, B, T], F32, name="gmn%d" % j) for j in range(G)]
         a_sc = [keep.tile([P, B, T], F32, name="a_sc%d" % j) for j in range(G)]
         b_sc = [keep.tile([P, B, T], F32, name="b_sc%d" % j) for j in range(G)]
         xb = [[keep.tile([P, T * HW], F32, name="xb%d_%d" % (b, j)) for j in range(G)] for b in range(B)]
-        sq = [keep.tile([P, NV], F32, name="sq%d" % j) for j in range(G)]
         tot = [keep.tile([P, B, 2], F32, name="tot%d" % j) for j in range(G)]
         msq = [keep.tile([P, B], F32, name="msq%d" % j) for j in range(G)]
         ve = [keep.tile([P, B], F32, name="ve%d" % j) for j in range(G)]
         sd = [keep.tile([P, B], F32, name="sd%d" % j) for j in range(G)]
         rstd = [keep.tile([P, B], F32, name="rstd%d" % j) for j in range(G)]
-        nmr = [keep.tile([P, B], F32, name="nmr%d" % j) for j in range(G)]
         bank = {}
 
         def y_view(j, b0, b1):
@@ -151,15 +153,15 @@ def tile_spatialcgnl_pb_kernel(tc, y, Wz, gamma, beta, x, out):
         def us(j, h, b, m):
             z = bank[("s", j, h, b, m)]
             if b < NV:
-                nc.vector.bn_stats(out=st[j][:, b, 2 * h + m, :], in_=z[:])
+                assert False
             else:
                 jk = junkp.tile([P, 512], BF16, name="jk")
                 nc.scalar.activation(out=jk[:], in_=z[:], func=ACT.Square,
-                                     accum_out=red[j][:, b, 1, 2 * h + m:2 * h + m + 1])
+                                     accum_out=st[j][:, NBN + 4 + 2 * h + m:NBN + 5 + 2 * h + m])
                 if (h, m) == (1, 1):
                     jk = junkp.tile([P, 512], BF16, name="jk")
                     nc.scalar.activation(out=jk[:], in_=bank[("a", j, b)][:], func=ACT.Identity,
-                                         accum_out=red[j][:, b, 0, 0:1])
+                                         accum_out=st[j][:, NBN:NBN + 1])
 
         def stat(j, h, b, m):
             ms(j, h, b, m)
@@ -169,53 +171,52 @@ def tile_spatialcgnl_pb_kernel(tc, y, Wz, gamma, beta, x, out):
             bank[("X", j, t)] = mm_apply(j, t, 0)
 
         def bna(j, t):
-            nc.vector.bn_stats(out=st[j][:, t, :], in_=bank[("X", j, t)][:].rearrange("p (i n) -> p n i", i=2))
+            nc.vector.bn_stats(out=st[j][:, 6 * t:6 * t + 6], in_=bank[("X", j, t)][:].rearrange("p (i n) -> p n i", i=2))
 
-        def ag(j, i):
-            nc.vector.bn_aggr(out=red[j][:, i, :, 0], in_=st[j][:, :, 3 * i:3 * i + 3])
+        def tik(ap):
+            return ap[:, 0:NBN].rearrange("p (t i k) -> p i t k", i=2, k=3)
 
-        def e2(j, i):
-            nc.vector.scalar_tensor_tensor(out=red[j][:, i, 1, 0:1], in0=red[j][:, i, 0, 0:1],
-                                           scalar=red[j][:, i, 0, 0:1], in1=red[j][:, i, 1, 0:1],
-                                           op0=ALU.mult, op1=ALU.add)
+        def ch(j, step):
+            gam_b = gam[:, j:j + 1, :].to_broadcast([P, B, T])
+            if step == 0:
+                v = tik(st[j])
+                nc.vector.scalar_tensor_tensor(out=v[:, :, :, 0], in0=v[:, :, :, 1], scalar=float(HW), in1=v[:, :, :, 1],
+                                               op0=ALU.mult, op1=ALU.mult)
+            elif step == 10:
+                v = tik(st[j])
+                nc.vector.tensor_scalar(out=v[:, :, :, 1], in0=v[:, :, :, 1], scalar1=float(HW), scalar2=0.0,
+                                        op0=ALU.mult, op1=ALU.add)
+            elif step == 1:
+                ps = bank[("c", j)]
+                nc.vector.tensor_reduce(out=tot[j][:, 0:2, 1], in_=tik(ps)[:, :, :, 0:3:2], axis=AX.XY, op=ALU.add)
+                nc.vector.tensor_reduce(out=tot[j][:, 0:2, 0], in_=tik(ps)[:, :, :, 1], axis=AX.X, op=ALU.add)
+                nc.vector.tensor_reduce(out=tot[j][:, 2, :], in_=ps[:, NBN:NST].rearrange("p (k f) -> p k f", f=4),
+                                        axis=AX.X, op=ALU.add)
+            elif step == 2:
+                nc.vector.scalar_tensor_tensor(out=msq[j][:], in0=tot[j][:, :, 0], scalar=-1.0, in1=tot[j][:, :, 0],
+                                               op0=ALU.mult, op1=ALU.mult)
+                nc.vector.scalar_tensor_tensor(out=gmn[j][:], in0=gam_b, scalar=-1.0,
+                                               in1=tot[j][:, :, 0].unsqueeze(2).to_broadcast([P, B, T]),
+                                               op0=ALU.mult, op1=ALU.mult)
+            elif step == 3:
+                nc.vector.scalar_tensor_tensor(out=ve[j][:], in0=tot[j][:, :, 1], scalar=EPS, in1=msq[j][:],
+                                               op0=ALU.add, op1=ALU.add)
+            elif step == 4:
+                nc.vector.reciprocal(out=rstd[j][:], in_=sd[j][:])
+            else:
+                for b in range(B):
+                    nc.vector.scalar_tensor_tensor(out=b_sc[j][:, b, :], in0=gmn[j][:, b, :], scalar=rstd[j][:, b:b + 1],
+                                                   in1=bet[:, j, :], op0=ALU.mult, op1=ALU.add)
+                nc.vector.tensor_tensor(out=a_sc[j][:], in0=gam_b,
+                                        in1=rstd[j][:].unsqueeze(2).to_broadcast([P, B, T]), op=ALU.mult)
 
         def cm(j):
-            ps = psum_s.tile([P, B, 2, 4], F32, name="ps")
+            ps = psum_s.tile([P, NST], F32, name="ps")
             bank[("c", j)] = ps
-            nc.tensor.matmul(ps[:, 0:NV].rearrange("p i k f -> p (i k f)"), lhsT=c_part[:],
-                             rhs=red[j][:, 0:NV].rearrange("p i k f -> p (i k f)"), start=True, stop=True)
-            nc.tensor.matmul(ps[:, NV:B].rearrange("p i k f -> p (i k f)"), lhsT=c_all[:],
-                             rhs=red[j][:, NV:B].rearrange("p i k f -> p (i k f)"), start=True, stop=True)
-
-        def c2(j, k):
-            if k == 0:
-                nc.vector.tensor_reduce(out=tot[j][:].rearrange("p i k -> p (i k)"),
-                                        in_=bank[("c", j)][:].rearrange("p i k f -> p (i k) f"), axis=AX.X, op=ALU.add)
-            elif k == 1:
-                nc.vector.tensor_tensor(out=msq[j][:], in0=tot[j][:, :, 0], in1=tot[j][:, :, 0], op=ALU.mult)
-            else:
-                nc.vector.scalar_tensor_tensor(out=ve[j][:], in0=tot[j][:, :, 1], scalar=EPS, in1=msq[j][:],
-                                               op0=ALU.add, op1=ALU.subtract)
+            nc.tensor.matmul(ps[:], lhsT=c_all[:], rhs=st[j][:], start=True, stop=True)
 
         def cs(j):
             nc.scalar.activation(out=sd[j][:], in_=ve[j][:], func=ACT.Sqrt)
-
-        def c3(j, k):
-            gam_b = gam[:, j:j + 1, :].to_broadcast([P, B, T])
-            bet_b = bet[:, j:j + 1, :].to_broadcast([P, B, T])
-            if k == 0:
-                nc.vector.reciprocal(out=rstd[j][:], in_=sd[j][:])
-            elif k == 1:
-                nc.vector.scalar_tensor_tensor(out=nmr[j][:], in0=tot[j][:, :, 0], scalar=-1.0, in1=rstd[j][:],
-                                               op0=ALU.mult, op1=ALU.mult)
-            elif k == 2:
-                nc.vector.tensor_tensor(out=a_sc[j][:], in0=gam_b,
-                                        in1=rstd[j][:].unsqueeze(2).to_broadcast([P, B, T]), op=ALU.mult)
-            elif k == 3:
-                nc.vector.tensor_tensor(out=b_sc[j][:], in0=gam_b,
-                                        in1=nmr[j][:].unsqueeze(2).to_broadcast([P, B, T]), op=ALU.mult)
-            else:
-                nc.vector.tensor_tensor(out=b_sc[j][:], in0=b_sc[j][:], in1=bet_b, op=ALU.add)
 
         def cols(t0, t1):
             return slice(t0 * HW, t1 * HW)
@@ -270,12 +271,11 @@ def tile_spatialcgnl_pb_kernel(tc, y, Wz, gamma, beta, x, out):
             nc.sync.dma_start(out=chan_view(out, b, j)[:, cols(t0, t1)], in_=xb[b][j][:, cols(t0, t1)])
 
         make_identity(nc, ident[:])
-        nc.gpsimd.memset(c_part[:], 1.0 / P)
         nc.gpsimd.memset(c_all[:], 1.0 / (CO * HW))
         nc.vector.memset(one[:], 1.0)
         nc.scalar.activation(out=warm[:], in_=one[:], func=ACT.Sqrt)
         for j in range(G):
-            nc.gpsimd.memset(red[j][:], 0.0)
+            nc.gpsimd.memset(st[j][:, NBN:NST], 0.0)
 
         ctx.enter_context(tc.manual_schedule())
 
@@ -346,21 +346,19 @@ def tile_spatialcgnl_pb_kernel(tc, y, Wz, gamma, beta, x, out):
             tr(1, s)
         for s in range(4):
             wc(1, s)
+        ch(0, 0)
         yi(1, 2, 3, "V")
-        ag(0, 0)
-        ag(0, 1)
-        yq(1, 2, 3)
-        e2(0, 0)
-        e2(0, 1)
+        ch(0, 10)
         cm(0)
+        yq(1, 2, 3)
         yq(1, 0, 2)
         wq(1, 0)
         wq(1, 1)
-        c2(0, 0)
+        ch(0, 1)
         wq(1, 2)
-        c2(0, 1)
+        ch(0, 2)
         wq(1, 3)
-        c2(0, 2)
+        ch(0, 3)
         cs(0)
 
         xq = [(b, t) for t in range(T) for b in range(2)]
@@ -375,22 +373,22 @@ def tile_spatialcgnl_pb_kernel(tc, y, Wz, gamma, beta, x, out):
                     xp(0, b, t, "S")
 
         SB = ((0, 0), (0, 1), (1, 0), (1, 1))
-        C3 = ((), (0,), (1, 2), (3,), (4,), (), (), ())
         for t in range(T):
             stat_a(1, t)
-            for k in C3[t]:
-                c3(0, k)
-                if k == 4:
-                    for tt in range(T):
-                        if not a2(tt):
-                            xp(0, 2, tt, "G")
+            if t == 1:
+                ch(0, 4)
+            if t == 2:
+                ch(0, 5)
+                for tt in range(T):
+                    if not a2(tt):
+                        xp(0, 2, tt, "G")
             if t % 2 == 1:
                 (h, m) = SB[t // 2]
                 stat_s(1, h, m)
-                if t >= 5:
-                    xpush(2)
+            if t >= XP0:
+                xpush(1)
 
-        CH = (("ag",), ("e2",), (), (), (), ("c2", 0), ("c2", 1), ("c2", 2), (), (), ("c3", 0), ("c3", 1, 2), ("c3", 3), ("c3", 4))
+        CH = (0, -1, 10, -1, -1, -1, 1, -1, -1, 2, -1, -1, 3, -1, -1, -1, 4, -1, -1, 5)
         issued = [0]
 
         def m_issue(n):
@@ -399,7 +397,7 @@ def tile_spatialcgnl_pb_kernel(tc, y, Wz, gamma, beta, x, out):
                 mb(0, issued[0])
                 issued[0] += 1
 
-        m_issue(2)
+        m_issue(3)
         hi = 0
         for t in range(T):
             if a2(t):
@@ -409,32 +407,27 @@ def tile_spatialcgnl_pb_kernel(tc, y, Wz, gamma, beta, x, out):
                 if hi < len(CH):
                     step = CH[hi]
                     hi += 1
-                    if step and step[0] == "ag":
-                        ag(1, 0)
-                        ag(1, 1)
-                    elif step and step[0] == "e2":
-                        e2(1, 0)
-                        e2(1, 1)
+                    if step >= 0:
+                        ch(1, step)
+                    if step == 10:
                         cm(1)
-                    elif step and step[0] == "c2":
-                        c2(1, step[1])
-                        if step[1] == 2:
-                            cs(1)
-                    elif step and step[0] == "c3":
-                        for k in step[1:]:
-                            c3(1, k)
+                    if step == 3:
+                        cs(1)
                 stt(0, b, t)
-                if hi == 2:
+                if hi == 1:
                     m_issue(3)
             m_issue(t + 3)
             xpush(2)
-            if t % 2 == 1:
+            if t < 2:
+                for b in range(2):
+                    so(0, b, t, t + 1)
+                if t == 1:
+                    so(0, 2, 0, 2)
+            elif t % 2 == 1:
                 for b in range(B):
                     so(0, b, t - 1, t + 1)
 
-        for t in range(T):
-            if not a2(t):
-                xp(1, 2, t, "G")
+        xp(1, 2, 1, "G")
 
         def xrow1(t):
             xp(1, 0, t, "S")
@@ -449,6 +442,8 @@ def tile_spatialcgnl_pb_kernel(tc, y, Wz, gamma, beta, x, out):
             if a2(t):
                 af(1, 2, t)
                 ga(1, 2, t, t + 1)
+                if t + 3 < T:
+                    xp(1, 2, t + 3, "G")
             if t + 2 < T:
                 xrow1(t + 2)
             for b in range(2 if a2(t) else B):

@@ -23,7 +23,10 @@ NWARM = 0
 NV = 2
 
 
-XP0 = 3
+EARLY = 2
+TE = 4
+XFIRST = 0
+CH = (0, -1, 10, -1, -1, 1, -1, 2, -1, 3, -1, -1, 4, -1, 5)
 
 
 def a2(t):
@@ -372,6 +375,40 @@ def tile_spatialcgnl_pb_kernel(tc, y, Wz, gamma, beta, x, out):
                     xn[0] += 1
                     xp(0, b, t, "S")
 
+        issued = [0]
+
+        def m_issue(n):
+            while issued[0] < min(n, T):
+                ma(0, issued[0])
+                mb(0, issued[0])
+                issued[0] += 1
+
+        hi = [0]
+
+        def row0(t, chain):
+            if a2(t):
+                af(0, 2, t)
+                ga(0, 2, t, t + 1)
+            for b in range(2 if a2(t) else B):
+                if chain and hi[0] < len(CH):
+                    step = CH[hi[0]]
+                    hi[0] += 1
+                    if step >= 0:
+                        ch(1, step)
+                    if step == 10:
+                        cm(1)
+                    if step == 3:
+                        cs(1)
+                stt(0, b, t)
+            if t < 2:
+                for b in range(2):
+                    so(0, b, t, t + 1)
+                if t == 1:
+                    so(0, 2, 0, 2)
+            elif t % 2 == 1:
+                for b in range(B):
+                    so(0, b, t - 1, t + 1)
+
         SB = ((0, 0), (0, 1), (1, 0), (1, 1))
         for t in range(T):
             stat_a(1, t)
@@ -382,50 +419,29 @@ def tile_spatialcgnl_pb_kernel(tc, y, Wz, gamma, beta, x, out):
                 for tt in range(T):
                     if not a2(tt):
                         xp(0, 2, tt, "G")
+                xpush(XFIRST)
             if t % 2 == 1:
                 (h, m) = SB[t // 2]
                 stat_s(1, h, m)
-            if t >= XP0:
+            if t > 2:
                 xpush(1)
+            if t == TE:
+                for r in range(EARLY):
+                    m_issue(r + 1)
+                    row0(r, False)
+                    xpush(2)
 
-        CH = (0, -1, 10, -1, -1, -1, 1, -1, -1, 2, -1, -1, 3, -1, -1, -1, 4, -1, -1, 5)
-        issued = [0]
-
-        def m_issue(n):
-            while issued[0] < min(n, T):
-                ma(0, issued[0])
-                mb(0, issued[0])
-                issued[0] += 1
-
-        m_issue(3)
-        hi = 0
-        for t in range(T):
-            if a2(t):
-                af(0, 2, t)
-                ga(0, 2, t, t + 1)
-            for b in range(2 if a2(t) else B):
-                if hi < len(CH):
-                    step = CH[hi]
-                    hi += 1
-                    if step >= 0:
-                        ch(1, step)
-                    if step == 10:
-                        cm(1)
-                    if step == 3:
-                        cs(1)
-                stt(0, b, t)
-                if hi == 1:
-                    m_issue(3)
+        m_issue(EARLY + 3)
+        for t in range(EARLY, T):
+            row0(t, True)
             m_issue(t + 3)
             xpush(2)
-            if t < 2:
-                for b in range(2):
-                    so(0, b, t, t + 1)
-                if t == 1:
-                    so(0, 2, 0, 2)
-            elif t % 2 == 1:
-                for b in range(B):
-                    so(0, b, t - 1, t + 1)
+        while hi[0] < len(CH):
+            if CH[hi[0]] >= 0:
+                ch(1, CH[hi[0]])
+            if CH[hi[0]] == 3:
+                cs(1)
+            hi[0] += 1
 
         xp(1, 2, 1, "G")
 

@@ -18,15 +18,15 @@ T = CO // P
 EPS = 1e-5
 FLOPS = 2 * B * G * CO * CG * HW
 NBN = 6 * T
-NST = NBN + 8
+NSC = NBN + 8
+NST = NSC + 2 * T
 NWARM = 0
 NV = 2
 
 
-EARLY = 2
-TE = 4
-XFIRST = 0
-CH = (0, -1, 10, -1, -1, 1, -1, 2, -1, 3, -1, -1, 4, -1, 5)
+PAT = (0, 0, 0, 3)
+CH = (0, -1, -1, -1, 1, -1, 2, -1, -1, 3)
+C0AT = 0
 
 
 def a2(t):
@@ -67,9 +67,7 @@ def tile_spatialcgnl_pb_kernel(tc, y, Wz, gamma, beta, x, out):
         b_sc = [keep.tile([P, B, T], F32, name="b_sc%d" % j) for j in range(G)]
         xb = [[keep.tile([P, T * HW], F32, name="xb%d_%d" % (b, j)) for j in range(G)] for b in range(B)]
         tot = [keep.tile([P, B, 2], F32, name="tot%d" % j) for j in range(G)]
-        msq = [keep.tile([P, B], F32, name="msq%d" % j) for j in range(G)]
         ve = [keep.tile([P, B], F32, name="ve%d" % j) for j in range(G)]
-        sd = [keep.tile([P, B], F32, name="sd%d" % j) for j in range(G)]
         rstd = [keep.tile([P, B], F32, name="rstd%d" % j) for j in range(G)]
         bank = {}
 
@@ -185,27 +183,22 @@ def tile_spatialcgnl_pb_kernel(tc, y, Wz, gamma, beta, x, out):
                 v = tik(st[j])
                 nc.vector.scalar_tensor_tensor(out=v[:, :, :, 0], in0=v[:, :, :, 1], scalar=float(HW), in1=v[:, :, :, 1],
                                                op0=ALU.mult, op1=ALU.mult)
-            elif step == 10:
-                v = tik(st[j])
-                nc.vector.tensor_scalar(out=v[:, :, :, 1], in0=v[:, :, :, 1], scalar1=float(HW), scalar2=0.0,
-                                        op0=ALU.mult, op1=ALU.add)
+                nc.vector.tensor_scalar(out=st[j][:, NSC:NST].rearrange("p (t i) -> p i t", i=2), in0=v[:, :, :, 1],
+                                        scalar1=float(HW), scalar2=0.0, op0=ALU.mult, op1=ALU.add)
             elif step == 1:
                 ps = bank[("c", j)]
                 nc.vector.tensor_reduce(out=tot[j][:, 0:2, 1], in_=tik(ps)[:, :, :, 0:3:2], axis=AX.XY, op=ALU.add)
-                nc.vector.tensor_reduce(out=tot[j][:, 0:2, 0], in_=tik(ps)[:, :, :, 1], axis=AX.X, op=ALU.add)
-                nc.vector.tensor_reduce(out=tot[j][:, 2, :], in_=ps[:, NBN:NST].rearrange("p (k f) -> p k f", f=4),
+                nc.vector.tensor_reduce(out=tot[j][:, 0:2, 0], in_=ps[:, NSC:NST].rearrange("p (t i) -> p i t", i=2),
+                                        axis=AX.X, op=ALU.add)
+                nc.vector.tensor_reduce(out=tot[j][:, 2, :], in_=ps[:, NBN:NSC].rearrange("p (k f) -> p k f", f=4),
                                         axis=AX.X, op=ALU.add)
             elif step == 2:
-                nc.vector.scalar_tensor_tensor(out=msq[j][:], in0=tot[j][:, :, 0], scalar=-1.0, in1=tot[j][:, :, 0],
-                                               op0=ALU.mult, op1=ALU.mult)
+                for b in range(B):
+                    nc.vector.scalar_tensor_tensor(out=ve[j][:, b:b + 1], in0=tot[j][:, b, 0:1], scalar=tot[j][:, b, 0:1],
+                                                   in1=tot[j][:, b, 1:2], op0=ALU.mult, op1=ALU.subtract)
                 nc.vector.scalar_tensor_tensor(out=gmn[j][:], in0=gam_b, scalar=-1.0,
                                                in1=tot[j][:, :, 0].unsqueeze(2).to_broadcast([P, B, T]),
                                                op0=ALU.mult, op1=ALU.mult)
-            elif step == 3:
-                nc.vector.scalar_tensor_tensor(out=ve[j][:], in0=tot[j][:, :, 1], scalar=EPS, in1=msq[j][:],
-                                               op0=ALU.add, op1=ALU.add)
-            elif step == 4:
-                nc.vector.reciprocal(out=rstd[j][:], in_=sd[j][:])
             else:
                 for b in range(B):
                     nc.vector.scalar_tensor_tensor(out=b_sc[j][:, b, :], in0=gmn[j][:, b, :], scalar=rstd[j][:, b:b + 1],
@@ -219,7 +212,7 @@ def tile_spatialcgnl_pb_kernel(tc, y, Wz, gamma, beta, x, out):
             nc.tensor.matmul(ps[:], lhsT=c_all[:], rhs=st[j][:], start=True, stop=True)
 
         def cs(j):
-            nc.scalar.activation(out=sd[j][:], in_=ve[j][:], func=ACT.Sqrt)
+            nc.scalar.activation(out=rstd[j][:], in_=ve[j][:], func=ACT.Abs_reciprocal_sqrt, bias=EPS, scale=-1.0)
 
         def cols(t0, t1):
             return slice(t0 * HW, t1 * HW)
@@ -276,9 +269,9 @@ def tile_spatialcgnl_pb_kernel(tc, y, Wz, gamma, beta, x, out):
         make_identity(nc, ident[:])
         nc.gpsimd.memset(c_all[:], 1.0 / (CO * HW))
         nc.vector.memset(one[:], 1.0)
-        nc.scalar.activation(out=warm[:], in_=one[:], func=ACT.Sqrt)
+        nc.scalar.activation(out=warm[:], in_=one[:], func=ACT.Abs_reciprocal_sqrt)
         for j in range(G):
-            nc.gpsimd.memset(st[j][:, NBN:NST], 0.0)
+            nc.gpsimd.memset(st[j][:, NBN:NSC], 0.0)
 
         ctx.enter_context(tc.manual_schedule())
 
@@ -350,9 +343,8 @@ def tile_spatialcgnl_pb_kernel(tc, y, Wz, gamma, beta, x, out):
         for s in range(4):
             wc(1, s)
         ch(0, 0)
-        yi(1, 2, 3, "V")
-        ch(0, 10)
         cm(0)
+        yi(1, 2, 3, "V")
         yq(1, 2, 3)
         yq(1, 0, 2)
         wq(1, 0)
@@ -360,9 +352,8 @@ def tile_spatialcgnl_pb_kernel(tc, y, Wz, gamma, beta, x, out):
         ch(0, 1)
         wq(1, 2)
         ch(0, 2)
-        wq(1, 3)
-        ch(0, 3)
         cs(0)
+        wq(1, 3)
 
         xq = [(b, t) for t in range(T) for b in range(2)]
 
@@ -384,6 +375,7 @@ def tile_spatialcgnl_pb_kernel(tc, y, Wz, gamma, beta, x, out):
                 issued[0] += 1
 
         hi = [0]
+        S0 = [(r, r + 1) for r in range(len(PAT))] + [(r, min(r + 2, T)) for r in range(len(PAT), T, 2)]
 
         def row0(t, chain):
             if a2(t):
@@ -395,51 +387,50 @@ def tile_spatialcgnl_pb_kernel(tc, y, Wz, gamma, beta, x, out):
                     hi[0] += 1
                     if step >= 0:
                         ch(1, step)
-                    if step == 10:
+                    if step == 0:
                         cm(1)
-                    if step == 3:
+                    if step == 2:
                         cs(1)
                 stt(0, b, t)
-            if t < 2:
-                for b in range(2):
-                    so(0, b, t, t + 1)
-                if t == 1:
-                    so(0, 2, 0, 2)
-            elif t % 2 == 1:
-                for b in range(B):
-                    so(0, b, t - 1, t + 1)
+            for (t0, t1) in S0:
+                if t == t1 - 1:
+                    for b in range(B):
+                        so(0, b, t0, t1)
 
         SB = ((0, 0), (0, 1), (1, 0), (1, 1))
-        for t in range(T):
+        def bank1(t):
             stat_a(1, t)
-            if t == 1:
-                ch(0, 4)
-            if t == 2:
-                ch(0, 5)
+            if t == C0AT:
+                ch(0, 3)
                 for tt in range(T):
                     if not a2(tt):
                         xp(0, 2, tt, "G")
-                xpush(XFIRST)
             if t % 2 == 1:
                 (h, m) = SB[t // 2]
                 stat_s(1, h, m)
-            if t > 2:
+            if t > C0AT:
                 xpush(1)
-            if t == TE:
-                for r in range(EARLY):
-                    m_issue(r + 1)
-                    row0(r, False)
-                    xpush(2)
 
-        m_issue(EARLY + 3)
-        for t in range(EARLY, T):
+        nbank = T - sum(PAT)
+        for t in range(nbank):
+            bank1(t)
+        for r in range(len(PAT)):
+            m_issue(r + 1)
+            row0(r, False)
+            xpush(2)
+            for i in range(PAT[r]):
+                bank1(nbank)
+                nbank += 1
+
+        m_issue(len(PAT) + 3)
+        for t in range(len(PAT), T):
             row0(t, True)
             m_issue(t + 3)
             xpush(2)
         while hi[0] < len(CH):
             if CH[hi[0]] >= 0:
                 ch(1, CH[hi[0]])
-            if CH[hi[0]] == 3:
+            if CH[hi[0]] == 2:
                 cs(1)
             hi[0] += 1
 

@@ -17,19 +17,19 @@ P = 128
 T = CO // P
 EPS = 1e-5
 FLOPS = 2 * B * G * CO * CG * HW
-NBN = 6 * T
-NSC = NBN + 8
-NST = NSC + 2 * T
-NWARM = 0
-NV = 2
+
+N_BN = 6 * T
+N_SC = N_BN + 8
+N_ST = N_SC + 2 * T
+
+EARLY_ROWS = 4
+LATE_BANKS = 3
+CHAIN_AT = (0, 4, 6, 9)
+ROWS_AHEAD = 3
+STORES_1 = ((0, 2), (2, 4), (4, 6), (6, 7), (7, 8))
 
 
-PAT = (0, 0, 0, 3)
-CH = (0, -1, -1, -1, 1, -1, 2, -1, -1, 3)
-C0AT = 0
-
-
-def a2(t):
+def by_scalar(t):
     return t % 2 == 0
 
 
@@ -58,56 +58,54 @@ def tile_spatialcgnl_pb_kernel(tc, y, Wz, gamma, beta, x, out):
         y_scl = [keep.tile([P, B * HW], U8, name="y_scl%d" % j, align_bytes=64) for j in range(G)]
         w_grp = [keep.tile([P, T * CG], BF16, name="w_grp0", tag="shared", align_bytes=64),
                  keep.tile([P, T * CG], BF16, name="w_grp1", align_bytes=64)]
-        wz = keep.tile([P, 512], BF16, name="wz")
         w_cod = [keep.tile([P, CO], U32, name="w_cod%d" % j, align_bytes=64) for j in range(G)]
         w_scl = [keep.tile([P, CO], U8, name="w_scl%d" % j, align_bytes=64) for j in range(G)]
-        st = [keep.tile([P, NST], F32, name="st%d" % j) for j in range(G)]
+        st = [keep.tile([P, N_ST], F32, name="st%d" % j) for j in range(G)]
         gmn = [keep.tile([P, B, T], F32, name="gmn%d" % j) for j in range(G)]
         a_sc = [keep.tile([P, B, T], F32, name="a_sc%d" % j) for j in range(G)]
         b_sc = [keep.tile([P, B, T], F32, name="b_sc%d" % j) for j in range(G)]
         xb = [[keep.tile([P, T * HW], F32, name="xb%d_%d" % (b, j)) for j in range(G)] for b in range(B)]
         tot = [keep.tile([P, B, 2], F32, name="tot%d" % j) for j in range(G)]
-        ve = [keep.tile([P, B], F32, name="ve%d" % j) for j in range(G)]
+        nvar = [keep.tile([P, B], F32, name="nvar%d" % j) for j in range(G)]
         rstd = [keep.tile([P, B], F32, name="rstd%d" % j) for j in range(G)]
         bank = {}
-
-        def y_view(j, b0, b1):
-            return y[b0:b1, j].rearrange("b (p q) w -> p b (q w)", q=4)
-
-        def w_view(j):
-            return Wz[j].rearrange("(p t) k -> p t k", t=T)
 
         def chan_view(ap, b, j):
             return ap[b].rearrange("(j p t) h w -> j p (t h w)", j=G, t=T)[j]
 
+        def cols(t0, t1):
+            return slice(t0 * HW, t1 * HW)
+
         def load_y(j, b0, b1):
-            nc.sync.dma_start(out=y_raw[j][:, b0:b1, :], in_=y_view(j, b0, b1))
+            nc.sync.dma_start(out=y_raw[j][:, b0:b1, :], in_=y[b0:b1, j].rearrange("b (p q) w -> p b (q w)", q=4))
 
         def load_w(j, t0, t1):
-            nc.sync.dma_start(out=w_raw[j][:, t0:t1, :], in_=w_view(j)[:, t0:t1, :])
+            nc.sync.dma_start(out=w_raw[j][:, t0:t1, :], in_=Wz[j].rearrange("(p t) k -> p t k", t=T)[:, t0:t1, :])
 
-        def yi(j, b0, b1, eng):
-            if eng == "G":
-                for b in range(b0, b1):
-                    nc.gpsimd.tensor_scalar(
-                        out=y_grp[j][:, b, :].rearrange("p (w q) -> p w q", q=4),
-                        in0=y_raw[j][:, b, :].rearrange("p (q w) -> p w q", q=4),
-                        scalar1=1.0, scalar2=0.0, op0=ALU.mult, op1=ALU.add,
-                    )
+        def store(j, b, t0, t1):
+            nc.sync.dma_start(out=chan_view(out, b, j)[:, cols(t0, t1)], in_=xb[b][j][:, cols(t0, t1)])
+
+        def interleave_y(j, b, on_gpsimd):
+            if on_gpsimd:
+                nc.gpsimd.tensor_scalar(
+                    out=y_grp[j][:, b, :].rearrange("p (w q) -> p w q", q=4),
+                    in0=y_raw[j][:, b, :].rearrange("p (q w) -> p w q", q=4),
+                    scalar1=1.0, scalar2=0.0, op0=ALU.mult, op1=ALU.add,
+                )
             else:
                 nc.vector.tensor_copy(
-                    out=y_grp[j][:, b0:b1, :].rearrange("p b (w q) -> p b w q", q=4),
-                    in_=y_raw[j][:, b0:b1, :].rearrange("p b (q w) -> p b w q", q=4),
+                    out=y_grp[j][:, b:b + 1, :].rearrange("p b (w q) -> p b w q", q=4),
+                    in_=y_raw[j][:, b:b + 1, :].rearrange("p b (q w) -> p b w q", q=4),
                 )
 
-        def yq(j, b0, b1):
+        def quantize_y(j, b0, b1):
             nc.vector.quantize_mx(
                 out=y_cod[j][:, b0 * HW:b1 * HW].bitcast(E5X4),
                 scales=y_scl[j][:, b0 * HW:b1 * HW],
                 in_=y_grp[j][:, b0:b1, :].rearrange("p b c -> p (b c)"),
             )
 
-        def tr(j, s):
+        def transpose_w(j, s):
             words = w_raw[j][:].bitcast(F32)
             z = psum_z.tile([P, 512], F32, name="z")
             bank[("t", j, s)] = z
@@ -116,117 +114,22 @@ def tile_spatialcgnl_pb_kernel(tc, y, Wz, gamma, beta, x, out):
                 for u in range(2):
                     nc.tensor.transpose(tp[:, tt, u, :], words[:, 2 * s + tt, u:CG // 2:2], ident[:])
 
-        def wc(j, s):
+        def copy_w(j, s):
             gwords = w_grp[j][:].bitcast(F32)
             nc.scalar.copy(
                 out=gwords[:, 512 * s:512 * (s + 1)].rearrange("p (s r u) -> p s r u", s=2, u=2),
                 in_=bank[("t", j, s)][:].rearrange("p (s u r) -> p s r u", s=2, u=2),
             )
 
-        def wq(j, s):
+        def quantize_w(j, s):
             nc.vector.quantize_mx(
                 out=w_cod[j][:, 256 * s:256 * (s + 1)].bitcast(E5X4),
                 scales=w_scl[j][:, 256 * s:256 * (s + 1)],
                 in_=w_grp[j][:, 1024 * s:1024 * (s + 1)],
             )
 
-        def mm_stat(z, j, b, m, h, start, stop):
-            c0 = b * HW + P * m
-            nc.tensor.matmul_mx(
-                out=z[:],
-                lhsT=y_cod[j][:, c0:c0 + P].bitcast(E5X4),
-                lhsT_scale=y_scl[j][:, c0:c0 + P],
-                rhs=w_cod[j][:, 512 * h:512 * (h + 1)].bitcast(E5X4),
-                rhs_scale=w_scl[j][:, 512 * h:512 * (h + 1)],
-                start=start,
-                stop=stop,
-            )
-
-        def ms(j, h, b, m):
-            z = psum_z.tile([P, 512], F32, name="z")
-            bank[("s", j, h, b, m)] = z
-            mm_stat(z, j, b, m, h, True, True)
-            if b >= NV:
-                if (h, m) == (0, 0):
-                    bank[("a", j, b)] = psum_a.tile([P, 512], F32, name="za")
-                mm_stat(bank[("a", j, b)], j, b, m, h, (h, m) == (0, 0), (h, m) == (1, 1))
-
-        def us(j, h, b, m):
-            z = bank[("s", j, h, b, m)]
-            if b < NV:
-                assert False
-            else:
-                jk = junkp.tile([P, 512], BF16, name="jk")
-                nc.scalar.activation(out=jk[:], in_=z[:], func=ACT.Square,
-                                     accum_out=st[j][:, NBN + 4 + 2 * h + m:NBN + 5 + 2 * h + m])
-                if (h, m) == (1, 1):
-                    jk = junkp.tile([P, 512], BF16, name="jk")
-                    nc.scalar.activation(out=jk[:], in_=bank[("a", j, b)][:], func=ACT.Identity,
-                                         accum_out=st[j][:, NBN:NBN + 1])
-
-        def stat(j, h, b, m):
-            ms(j, h, b, m)
-            us(j, h, b, m)
-
-        def mx(j, t):
-            bank[("X", j, t)] = mm_apply(j, t, 0)
-
-        def bna(j, t):
-            nc.vector.bn_stats(out=st[j][:, 6 * t:6 * t + 6], in_=bank[("X", j, t)][:].rearrange("p (i n) -> p n i", i=2))
-
-        def tik(ap):
-            return ap[:, 0:NBN].rearrange("p (t i k) -> p i t k", i=2, k=3)
-
-        def ch(j, step):
-            gam_b = gam[:, j:j + 1, :].to_broadcast([P, B, T])
-            if step == 0:
-                v = tik(st[j])
-                nc.vector.scalar_tensor_tensor(out=v[:, :, :, 0], in0=v[:, :, :, 1], scalar=float(HW), in1=v[:, :, :, 1],
-                                               op0=ALU.mult, op1=ALU.mult)
-                nc.vector.tensor_scalar(out=st[j][:, NSC:NST].rearrange("p (t i) -> p i t", i=2), in0=v[:, :, :, 1],
-                                        scalar1=float(HW), scalar2=0.0, op0=ALU.mult, op1=ALU.add)
-            elif step == 1:
-                ps = bank[("c", j)]
-                nc.vector.tensor_reduce(out=tot[j][:, 0:2, 1], in_=tik(ps)[:, :, :, 0:3:2], axis=AX.XY, op=ALU.add)
-                nc.vector.tensor_reduce(out=tot[j][:, 0:2, 0], in_=ps[:, NSC:NST].rearrange("p (t i) -> p i t", i=2),
-                                        axis=AX.X, op=ALU.add)
-                nc.vector.tensor_reduce(out=tot[j][:, 2, :], in_=ps[:, NBN:NSC].rearrange("p (k f) -> p k f", f=4),
-                                        axis=AX.X, op=ALU.add)
-            elif step == 2:
-                for b in range(B):
-                    nc.vector.scalar_tensor_tensor(out=ve[j][:, b:b + 1], in0=tot[j][:, b, 0:1], scalar=tot[j][:, b, 0:1],
-                                                   in1=tot[j][:, b, 1:2], op0=ALU.mult, op1=ALU.subtract)
-                nc.vector.scalar_tensor_tensor(out=gmn[j][:], in0=gam_b, scalar=-1.0,
-                                               in1=tot[j][:, :, 0].unsqueeze(2).to_broadcast([P, B, T]),
-                                               op0=ALU.mult, op1=ALU.mult)
-            else:
-                for b in range(B):
-                    nc.vector.scalar_tensor_tensor(out=b_sc[j][:, b, :], in0=gmn[j][:, b, :], scalar=rstd[j][:, b:b + 1],
-                                                   in1=bet[:, j, :], op0=ALU.mult, op1=ALU.add)
-                nc.vector.tensor_tensor(out=a_sc[j][:], in0=gam_b,
-                                        in1=rstd[j][:].unsqueeze(2).to_broadcast([P, B, T]), op=ALU.mult)
-
-        def cm(j):
-            ps = psum_s.tile([P, NST], F32, name="ps")
-            bank[("c", j)] = ps
-            nc.tensor.matmul(ps[:], lhsT=c_all[:], rhs=st[j][:], start=True, stop=True)
-
-        def cs(j):
-            nc.scalar.activation(out=rstd[j][:], in_=ve[j][:], func=ACT.Abs_reciprocal_sqrt, bias=EPS, scale=-1.0)
-
-        def cols(t0, t1):
-            return slice(t0 * HW, t1 * HW)
-
-        def xp(j, b, t, eng):
-            if eng == "G":
-                nc.gpsimd.tensor_scalar(out=xb[b][j][:, cols(t, t + 1)], in0=x_sb[b][j][:, cols(t, t + 1)],
-                                        scalar1=one[:, 0:1], scalar2=b_sc[j][:, b, t:t + 1],
-                                        op0=ALU.mult, op1=ALU.add)
-            else:
-                nc.scalar.activation(out=xb[b][j][:, cols(t, t + 1)], in_=x_sb[b][j][:, cols(t, t + 1)],
-                                     func=ACT.Identity, bias=b_sc[j][:, b, t:t + 1], scale=1.0)
-
-        def mm_apply(j, t, c0):
+        def product(j, t, first_image):
+            c0 = first_image * HW
             z = psum_z.tile([P, 512], F32, name="z")
             nc.tensor.matmul_mx(
                 out=z[:],
@@ -239,39 +142,116 @@ def tile_spatialcgnl_pb_kernel(tc, y, Wz, gamma, beta, x, out):
             )
             return z
 
-        def ma(j, t):
-            bank[("A", j, t)] = mm_apply(j, t, 0)
+        def position_pass(z, j, m, h, start, stop):
+            c0 = 2 * HW + P * m
+            nc.tensor.matmul_mx(
+                out=z[:],
+                lhsT=y_cod[j][:, c0:c0 + P].bitcast(E5X4),
+                lhsT_scale=y_scl[j][:, c0:c0 + P],
+                rhs=w_cod[j][:, 512 * h:512 * (h + 1)].bitcast(E5X4),
+                rhs_scale=w_scl[j][:, 512 * h:512 * (h + 1)],
+                start=start,
+                stop=stop,
+            )
 
-        def mb(j, t):
-            bank[("B", j, t)] = mm_apply(j, t, HW)
+        def pair_product(j, t):
+            bank[("X", j, t)] = product(j, t, 0)
 
-        def zhalf(j, b, t):
+        def pair_bn(j, t):
+            nc.vector.bn_stats(out=st[j][:, 6 * t:6 * t + 6],
+                               in_=bank[("X", j, t)][:].rearrange("p (i n) -> p n i", i=2))
+
+        def pair_stats(j, t):
+            pair_product(j, t)
+            pair_bn(j, t)
+
+        def image2_stats(j, k):
+            (h, m) = (k // 2, k % 2)
+            z = psum_z.tile([P, 512], F32, name="z")
+            position_pass(z, j, m, h, True, True)
+            if k == 0:
+                bank[("a", j)] = psum_a.tile([P, 512], F32, name="za")
+            position_pass(bank[("a", j)], j, m, h, k == 0, k == 3)
+            jk = junkp.tile([P, 512], BF16, name="jk")
+            nc.scalar.activation(out=jk[:], in_=z[:], func=ACT.Square, accum_out=st[j][:, N_BN + 4 + k:N_BN + 5 + k])
+            if k == 3:
+                jk = junkp.tile([P, 512], BF16, name="jk")
+                nc.scalar.activation(out=jk[:], in_=bank[("a", j)][:], func=ACT.Identity,
+                                     accum_out=st[j][:, N_BN:N_BN + 1])
+
+        def bn_view(ap):
+            return ap[:, 0:N_BN].rearrange("p (t i k) -> p i t k", i=2, k=3)
+
+        def chain(j, step):
+            gam_b = gam[:, j:j + 1, :].to_broadcast([P, B, T])
+            if step == 0:
+                v = bn_view(st[j])
+                nc.vector.scalar_tensor_tensor(out=v[:, :, :, 0], in0=v[:, :, :, 1], scalar=float(HW),
+                                               in1=v[:, :, :, 1], op0=ALU.mult, op1=ALU.mult)
+                nc.vector.tensor_scalar(out=st[j][:, N_SC:N_ST].rearrange("p (t i) -> p i t", i=2), in0=v[:, :, :, 1],
+                                        scalar1=float(HW), scalar2=0.0, op0=ALU.mult, op1=ALU.add)
+                ps = psum_s.tile([P, N_ST], F32, name="ps")
+                bank[("c", j)] = ps
+                nc.tensor.matmul(ps[:], lhsT=c_all[:], rhs=st[j][:], start=True, stop=True)
+            elif step == 1:
+                ps = bank[("c", j)]
+                nc.vector.tensor_reduce(out=tot[j][:, 0:2, 1], in_=bn_view(ps)[:, :, :, 0:3:2], axis=AX.XY, op=ALU.add)
+                nc.vector.tensor_reduce(out=tot[j][:, 0:2, 0], in_=ps[:, N_SC:N_ST].rearrange("p (t i) -> p i t", i=2),
+                                        axis=AX.X, op=ALU.add)
+                nc.vector.tensor_reduce(out=tot[j][:, 2, :], in_=ps[:, N_BN:N_SC].rearrange("p (k f) -> p k f", f=4),
+                                        axis=AX.X, op=ALU.add)
+            elif step == 2:
+                for b in range(B):
+                    nc.vector.scalar_tensor_tensor(out=nvar[j][:, b:b + 1], in0=tot[j][:, b, 0:1],
+                                                   scalar=tot[j][:, b, 0:1], in1=tot[j][:, b, 1:2],
+                                                   op0=ALU.mult, op1=ALU.subtract)
+                nc.vector.scalar_tensor_tensor(out=gmn[j][:], in0=gam_b, scalar=-1.0,
+                                               in1=tot[j][:, :, 0].unsqueeze(2).to_broadcast([P, B, T]),
+                                               op0=ALU.mult, op1=ALU.mult)
+                nc.scalar.activation(out=rstd[j][:], in_=nvar[j][:], func=ACT.Abs_reciprocal_sqrt, bias=EPS, scale=-1.0)
+            else:
+                for b in range(B):
+                    nc.vector.scalar_tensor_tensor(out=b_sc[j][:, b, :], in0=gmn[j][:, b, :],
+                                                   scalar=rstd[j][:, b:b + 1], in1=bet[:, j, :],
+                                                   op0=ALU.mult, op1=ALU.add)
+                nc.vector.tensor_tensor(out=a_sc[j][:], in0=gam_b,
+                                        in1=rstd[j][:].unsqueeze(2).to_broadcast([P, B, T]), op=ALU.mult)
+
+        def row_products(j, t):
+            bank[("A", j, t)] = product(j, t, 0)
+            bank[("B", j, t)] = product(j, t, 1)
+
+        def z_of(j, b, t):
             if b < 2:
                 return bank[("A", j, t)][:, b * HW:(b + 1) * HW]
             return bank[("B", j, t)][:, HW:2 * HW]
 
-        def stt(j, b, t):
-            nc.vector.scalar_tensor_tensor(out=xb[b][j][:, cols(t, t + 1)], in0=zhalf(j, b, t),
+        def x_plus_b(j, b, t, on_gpsimd):
+            if on_gpsimd:
+                nc.gpsimd.tensor_scalar(out=xb[b][j][:, cols(t, t + 1)], in0=x_sb[b][j][:, cols(t, t + 1)],
+                                        scalar1=one[:, 0:1], scalar2=b_sc[j][:, b, t:t + 1],
+                                        op0=ALU.mult, op1=ALU.add)
+            else:
+                nc.scalar.activation(out=xb[b][j][:, cols(t, t + 1)], in_=x_sb[b][j][:, cols(t, t + 1)],
+                                     func=ACT.Identity, bias=b_sc[j][:, b, t:t + 1], scale=1.0)
+
+        def vector_tile(j, b, t):
+            nc.vector.scalar_tensor_tensor(out=xb[b][j][:, cols(t, t + 1)], in0=z_of(j, b, t),
                                            scalar=a_sc[j][:, b, t:t + 1], in1=xb[b][j][:, cols(t, t + 1)],
                                            op0=ALU.mult, op1=ALU.add)
 
-        def af(j, b, t):
-            nc.scalar.activation(out=xb[b][j][:, cols(t, t + 1)], in_=zhalf(j, b, t), func=ACT.Identity,
-                                 bias=b_sc[j][:, b, t:t + 1], scale=a_sc[j][:, b, t:t + 1])
-
-        def ga(j, b, t0, t1):
-            nc.gpsimd.tensor_tensor(out=xb[b][j][:, cols(t0, t1)], in0=xb[b][j][:, cols(t0, t1)],
-                                    in1=x_sb[b][j][:, cols(t0, t1)], op=ALU.add)
-
-        def so(j, b, t0, t1):
-            nc.sync.dma_start(out=chan_view(out, b, j)[:, cols(t0, t1)], in_=xb[b][j][:, cols(t0, t1)])
+        def scalar_gpsimd_tile(j, t):
+            nc.scalar.activation(out=xb[2][j][:, cols(t, t + 1)], in_=z_of(j, 2, t), func=ACT.Identity,
+                                 bias=b_sc[j][:, 2, t:t + 1], scale=a_sc[j][:, 2, t:t + 1])
+            nc.gpsimd.tensor_tensor(out=xb[2][j][:, cols(t, t + 1)], in0=xb[2][j][:, cols(t, t + 1)],
+                                    in1=x_sb[2][j][:, cols(t, t + 1)], op=ALU.add)
 
         make_identity(nc, ident[:])
         nc.gpsimd.memset(c_all[:], 1.0 / (CO * HW))
         nc.vector.memset(one[:], 1.0)
         nc.scalar.activation(out=warm[:], in_=one[:], func=ACT.Abs_reciprocal_sqrt)
         for j in range(G):
-            nc.gpsimd.memset(st[j][:, NBN:NSC], 0.0)
+            nc.gpsimd.memset(st[j][:, N_BN:N_SC], 0.0)
 
         ctx.enter_context(tc.manual_schedule())
 
@@ -291,171 +271,134 @@ def tile_spatialcgnl_pb_kernel(tc, y, Wz, gamma, beta, x, out):
             for b in range(B):
                 nc.sync.dma_start(out=x_sb[b][j][:], in_=chan_view(x, b, j))
 
-
-        def stat_a(j, t):
-            mx(j, t)
-            bna(j, t)
-
-        def stat_s(j, h, m):
-            ms(j, h, 2, m)
-            us(j, h, 2, m)
-
-        yi(0, 0, 1, "V")
-        yi(0, 1, 2, "V")
-        yq(0, 0, 2)
-        tr(0, 0)
-        wc(0, 0)
-        tr(0, 1)
-        wc(0, 1)
-        wq(0, 0)
-        yi(0, 2, 3, "V")
-        yq(0, 2, 3)
-        wq(0, 1)
-        mx(0, 0)
-        mx(0, 1)
-        tr(0, 2)
-        wc(0, 2)
-        mx(0, 2)
-        mx(0, 3)
-        tr(0, 3)
-        wc(0, 3)
-        bna(0, 0)
-        bna(0, 1)
-        wq(0, 2)
-        bna(0, 2)
-        bna(0, 3)
-        wq(0, 3)
+        interleave_y(0, 0, False)
+        interleave_y(0, 1, False)
+        quantize_y(0, 0, 2)
+        transpose_w(0, 0)
+        copy_w(0, 0)
+        transpose_w(0, 1)
+        copy_w(0, 1)
+        quantize_w(0, 0)
+        interleave_y(0, 2, False)
+        quantize_y(0, 2, 3)
+        quantize_w(0, 1)
+        pair_product(0, 0)
+        pair_product(0, 1)
+        transpose_w(0, 2)
+        copy_w(0, 2)
+        pair_product(0, 2)
+        pair_product(0, 3)
+        transpose_w(0, 3)
+        copy_w(0, 3)
+        pair_bn(0, 0)
+        pair_bn(0, 1)
+        quantize_w(0, 2)
+        pair_bn(0, 2)
+        pair_bn(0, 3)
+        quantize_w(0, 3)
         y_grp[1] = keep.tile([P, B, 4 * HW], BF16, name="y_grp1", tag="shared", align_bytes=64)
-        yi(1, 0, 2, "G")
+        interleave_y(1, 0, True)
+        interleave_y(1, 1, True)
         nc.gpsimd.tensor_copy(out=gam[:], in_=g_bf[:])
         nc.gpsimd.tensor_copy(out=bet[:], in_=b_bf[:])
-        stat_s(0, 0, 0)
-        stat_a(0, 4)
-        stat_s(0, 0, 1)
-        stat_a(0, 5)
-        stat_s(0, 1, 0)
-        stat_a(0, 6)
-        stat_s(0, 1, 1)
-        stat_a(0, 7)
+        for k in range(4):
+            image2_stats(0, k)
+            pair_stats(0, 4 + k)
 
         for s in range(4):
-            tr(1, s)
+            transpose_w(1, s)
         for s in range(4):
-            wc(1, s)
-        ch(0, 0)
-        cm(0)
-        yi(1, 2, 3, "V")
-        yq(1, 2, 3)
-        yq(1, 0, 2)
-        wq(1, 0)
-        wq(1, 1)
-        ch(0, 1)
-        wq(1, 2)
-        ch(0, 2)
-        cs(0)
-        wq(1, 3)
+            copy_w(1, s)
+        chain(0, 0)
+        interleave_y(1, 2, False)
+        quantize_y(1, 2, 3)
+        quantize_y(1, 0, 2)
+        quantize_w(1, 0)
+        quantize_w(1, 1)
+        chain(0, 1)
+        quantize_w(1, 2)
+        chain(0, 2)
+        quantize_w(1, 3)
 
-        xq = [(b, t) for t in range(T) for b in range(2)]
+        scalar_tiles = [(b, t) for t in range(T) for b in range(2)]
+        scalar_done = [0]
 
-        xn = [0]
-
-        def xpush(n):
+        def scalar_x_plus_b(n):
             for i in range(n):
-                if xn[0] < len(xq):
-                    (b, t) = xq[xn[0]]
-                    xn[0] += 1
-                    xp(0, b, t, "S")
+                if scalar_done[0] < len(scalar_tiles):
+                    (b, t) = scalar_tiles[scalar_done[0]]
+                    scalar_done[0] += 1
+                    x_plus_b(0, b, t, False)
 
-        issued = [0]
+        rows_written = [0]
 
-        def m_issue(n):
-            while issued[0] < min(n, T):
-                ma(0, issued[0])
-                mb(0, issued[0])
-                issued[0] += 1
+        def products_up_to(n):
+            while rows_written[0] < min(n, T):
+                row_products(0, rows_written[0])
+                rows_written[0] += 1
 
-        hi = [0]
-        S0 = [(r, r + 1) for r in range(len(PAT))] + [(r, min(r + 2, T)) for r in range(len(PAT), T, 2)]
+        stores_0 = [(r, r + 1) for r in range(EARLY_ROWS)] + [(r, r + 2) for r in range(EARLY_ROWS, T, 2)]
+        tiles_done = [0]
 
-        def row0(t, chain):
-            if a2(t):
-                af(0, 2, t)
-                ga(0, 2, t, t + 1)
-            for b in range(2 if a2(t) else B):
-                if chain and hi[0] < len(CH):
-                    step = CH[hi[0]]
-                    hi[0] += 1
-                    if step >= 0:
-                        ch(1, step)
-                    if step == 0:
-                        cm(1)
-                    if step == 2:
-                        cs(1)
-                stt(0, b, t)
-            for (t0, t1) in S0:
+        def row_0(t, with_chain):
+            if by_scalar(t):
+                scalar_gpsimd_tile(0, t)
+            for b in range(2 if by_scalar(t) else B):
+                if with_chain:
+                    for k in range(len(CHAIN_AT)):
+                        if CHAIN_AT[k] == tiles_done[0]:
+                            chain(1, k)
+                    tiles_done[0] += 1
+                vector_tile(0, b, t)
+            for (t0, t1) in stores_0:
                 if t == t1 - 1:
                     for b in range(B):
-                        so(0, b, t0, t1)
+                        store(0, b, t0, t1)
 
-        SB = ((0, 0), (0, 1), (1, 0), (1, 1))
-        def bank1(t):
-            stat_a(1, t)
-            if t == C0AT:
-                ch(0, 3)
+        def bank_1(t):
+            pair_stats(1, t)
+            if t == 0:
+                chain(0, 3)
                 for tt in range(T):
-                    if not a2(tt):
-                        xp(0, 2, tt, "G")
+                    if not by_scalar(tt):
+                        x_plus_b(0, 2, tt, True)
             if t % 2 == 1:
-                (h, m) = SB[t // 2]
-                stat_s(1, h, m)
-            if t > C0AT:
-                xpush(1)
+                image2_stats(1, t // 2)
+            if t > 0:
+                scalar_x_plus_b(1)
 
-        nbank = T - sum(PAT)
-        for t in range(nbank):
-            bank1(t)
-        for r in range(len(PAT)):
-            m_issue(r + 1)
-            row0(r, False)
-            xpush(2)
-            for i in range(PAT[r]):
-                bank1(nbank)
-                nbank += 1
+        for t in range(T - LATE_BANKS):
+            bank_1(t)
+        for t in range(EARLY_ROWS):
+            products_up_to(t + 1)
+            row_0(t, False)
+            scalar_x_plus_b(2)
+        for t in range(T - LATE_BANKS, T):
+            bank_1(t)
+        products_up_to(EARLY_ROWS + ROWS_AHEAD)
+        for t in range(EARLY_ROWS, T):
+            row_0(t, True)
+            products_up_to(t + ROWS_AHEAD)
+            scalar_x_plus_b(2)
 
-        m_issue(len(PAT) + 3)
-        for t in range(len(PAT), T):
-            row0(t, True)
-            m_issue(t + 3)
-            xpush(2)
-        while hi[0] < len(CH):
-            if CH[hi[0]] >= 0:
-                ch(1, CH[hi[0]])
-            if CH[hi[0]] == 2:
-                cs(1)
-            hi[0] += 1
+        def scalar_row_1(t):
+            x_plus_b(1, 0, t, False)
+            x_plus_b(1, 1, t, False)
 
-        xp(1, 2, 1, "G")
-
-        def xrow1(t):
-            xp(1, 0, t, "S")
-            xp(1, 1, t, "S")
-
-        xrow1(0)
-        xrow1(1)
-        STORES = ((0, 2), (2, 4), (4, 6), (6, 7), (7, 8))
+        x_plus_b(1, 2, 1, True)
+        scalar_row_1(0)
+        scalar_row_1(1)
         for t in range(T):
-            ma(1, t)
-            mb(1, t)
-            if a2(t):
-                af(1, 2, t)
-                ga(1, 2, t, t + 1)
+            row_products(1, t)
+            if by_scalar(t):
+                scalar_gpsimd_tile(1, t)
                 if t + 3 < T:
-                    xp(1, 2, t + 3, "G")
+                    x_plus_b(1, 2, t + 3, True)
             if t + 2 < T:
-                xrow1(t + 2)
-            for b in range(2 if a2(t) else B):
-                stt(1, b, t)
-            for (t0, t1) in STORES:
+                scalar_row_1(t + 2)
+            for b in range(2 if by_scalar(t) else B):
+                vector_tile(1, b, t)
+            for (t0, t1) in STORES_1:
                 if t == t1 - 1:
                     for b in range(B):
-                        so(1, b, t0, t1)
+                        store(1, b, t0, t1)

@@ -273,13 +273,14 @@ def tile_spatialcgnl_pb_kernel(tc, y, Wz, gamma, beta, x, out):
 
         interleave_y(0, 0, False)
         interleave_y(0, 1, False)
-        quantize_y(0, 0, 2)
+        quantize_y(0, 0, 1)
+        quantize_y(0, 1, 2)
         transpose_w(0, 0)
         copy_w(0, 0)
         transpose_w(0, 1)
         copy_w(0, 1)
-        quantize_w(0, 0)
         interleave_y(0, 2, False)
+        quantize_w(0, 0)
         quantize_y(0, 2, 3)
         quantize_w(0, 1)
         pair_product(0, 0)
@@ -311,8 +312,8 @@ def tile_spatialcgnl_pb_kernel(tc, y, Wz, gamma, beta, x, out):
             copy_w(1, s)
         chain(0, 0)
         interleave_y(1, 2, False)
-        quantize_y(1, 2, 3)
         quantize_y(1, 0, 2)
+        quantize_y(1, 2, 3)
         quantize_w(1, 0)
         quantize_w(1, 1)
         chain(0, 1)

@@ -24,7 +24,7 @@ N_ST = N_SC + 2 * T
 
 EARLY_ROWS = 4
 LATE_BANKS = 3
-CHAIN_AT = (0, 4, 6, 9)
+CHAIN_AT = (1, 5, 7, 9)
 ROWS_AHEAD = 3
 STORES_1 = ((0, 2), (2, 4), (4, 6), (6, 7), (7, 8))
 
@@ -279,18 +279,18 @@ def tile_spatialcgnl_pb_kernel(tc, y, Wz, gamma, beta, x, out):
         copy_w(0, 0)
         transpose_w(0, 1)
         copy_w(0, 1)
+        transpose_w(0, 2)
+        copy_w(0, 2)
         interleave_y(0, 2, False)
         quantize_w(0, 0)
         quantize_y(0, 2, 3)
         quantize_w(0, 1)
         pair_product(0, 0)
         pair_product(0, 1)
-        transpose_w(0, 2)
-        copy_w(0, 2)
-        pair_product(0, 2)
-        pair_product(0, 3)
         transpose_w(0, 3)
         copy_w(0, 3)
+        pair_product(0, 2)
+        pair_product(0, 3)
         pair_bn(0, 0)
         pair_bn(0, 1)
         quantize_w(0, 2)
@@ -302,17 +302,23 @@ def tile_spatialcgnl_pb_kernel(tc, y, Wz, gamma, beta, x, out):
         interleave_y(1, 1, True)
         nc.gpsimd.tensor_copy(out=gam[:], in_=g_bf[:])
         nc.gpsimd.tensor_copy(out=bet[:], in_=b_bf[:])
-        for k in range(4):
-            image2_stats(0, k)
-            pair_stats(0, 4 + k)
+        image2_stats(0, 0)
+        image2_stats(0, 1)
+        pair_stats(0, 4)
+        pair_stats(0, 5)
+        image2_stats(0, 2)
+        pair_stats(0, 6)
+        pair_stats(0, 7)
+        image2_stats(0, 3)
 
         for s in range(4):
             transpose_w(1, s)
         for s in range(4):
             copy_w(1, s)
+        quantize_y(1, 0, 1)
         chain(0, 0)
         interleave_y(1, 2, False)
-        quantize_y(1, 0, 2)
+        quantize_y(1, 1, 2)
         quantize_y(1, 2, 3)
         quantize_w(1, 0)
         quantize_w(1, 1)

@@ -49,10 +49,8 @@ def tile_spatialcgnl_pb_kernel(tc, y, Wz, gamma, beta, x, out):
         y_raw = [keep.tile([P, B, 4 * HW], BF16, name="y_raw%d" % j) for j in range(G)]
         w_raw = [keep.tile([P, T, CG], BF16, name="w_raw%d" % j) for j in range(G)]
         x_sb = [[keep.tile([P, T * HW], BF16, name="x_sb%d_%d" % (b, j)) for j in range(G)] for b in range(B)]
-        g_bf = keep.tile([P, G, T], BF16, name="g_bf")
-        b_bf = keep.tile([P, G, T], BF16, name="b_bf")
-        gam = keep.tile([P, G, T], F32, name="gam")
-        bet = keep.tile([P, G, T], F32, name="bet")
+        gam = keep.tile([P, G, T], BF16, name="gam")
+        bet = keep.tile([P, G, T], BF16, name="bet")
         y_grp = [keep.tile([P, B, 4 * HW], BF16, name="y_grp0", align_bytes=64), None]
         y_cod = [keep.tile([P, B * HW], U32, name="y_cod%d" % j, align_bytes=64) for j in range(G)]
         y_scl = [keep.tile([P, B * HW], U8, name="y_scl%d" % j, align_bytes=64) for j in range(G)]
@@ -265,8 +263,8 @@ def tile_spatialcgnl_pb_kernel(tc, y, Wz, gamma, beta, x, out):
         load_y(1, 0, 3)
         load_w(1, 0, 4)
         load_w(1, 4, 8)
-        nc.sync.dma_start(out=g_bf[:], in_=gamma.rearrange("(j p t) -> p j t", j=G, t=T))
-        nc.sync.dma_start(out=b_bf[:], in_=beta.rearrange("(j p t) -> p j t", j=G, t=T))
+        nc.sync.dma_start(out=gam[:], in_=gamma.rearrange("(j p t) -> p j t", j=G, t=T))
+        nc.sync.dma_start(out=bet[:], in_=beta.rearrange("(j p t) -> p j t", j=G, t=T))
         for j in range(G):
             for b in range(B):
                 nc.sync.dma_start(out=x_sb[b][j][:], in_=chan_view(x, b, j))
@@ -292,16 +290,14 @@ def tile_spatialcgnl_pb_kernel(tc, y, Wz, gamma, beta, x, out):
         pair_product(0, 2)
         pair_product(0, 3)
         pair_bn(0, 0)
-        pair_bn(0, 1)
         quantize_w(0, 2)
-        pair_bn(0, 2)
-        pair_bn(0, 3)
+        pair_bn(0, 1)
         quantize_w(0, 3)
         y_grp[1] = keep.tile([P, B, 4 * HW], BF16, name="y_grp1", tag="shared", align_bytes=64)
         interleave_y(1, 0, True)
         interleave_y(1, 1, True)
-        nc.gpsimd.tensor_copy(out=gam[:], in_=g_bf[:])
-        nc.gpsimd.tensor_copy(out=bet[:], in_=b_bf[:])
+        pair_bn(0, 2)
+        pair_bn(0, 3)
         image2_stats(0, 0)
         image2_stats(0, 1)
         pair_stats(0, 4)

@@ -24,13 +24,13 @@ N_ST = N_SC + 2 * T
 
 EARLY_ROWS = 4
 LATE_BANKS = 3
-CHAIN_AT = (1, 5, 7, 9)
+CHAIN_AT = (1, 6, 8, 10)
 ROWS_AHEAD = 3
 STORES_1 = ((0, 2), (2, 4), (4, 6), (6, 7), (7, 8))
 
 
-def by_scalar(t):
-    return t % 2 == 0
+def by_scalar(j, t):
+    return t < EARLY_ROWS if j == 0 else t % 2 == 0
 
 
 def tile_spatialcgnl_pb_kernel(tc, y, Wz, gamma, beta, x, out):
@@ -344,9 +344,9 @@ def tile_spatialcgnl_pb_kernel(tc, y, Wz, gamma, beta, x, out):
         tiles_done = [0]
 
         def row_0(t, with_chain):
-            if by_scalar(t):
+            if by_scalar(0, t):
                 scalar_gpsimd_tile(0, t)
-            for b in range(2 if by_scalar(t) else B):
+            for b in range(2 if by_scalar(0, t) else B):
                 if with_chain:
                     for k in range(len(CHAIN_AT)):
                         if CHAIN_AT[k] == tiles_done[0]:
@@ -363,7 +363,7 @@ def tile_spatialcgnl_pb_kernel(tc, y, Wz, gamma, beta, x, out):
             if t == 0:
                 chain(0, 3)
                 for tt in range(T):
-                    if not by_scalar(tt):
+                    if not by_scalar(0, tt):
                         x_plus_b(0, 2, tt, True)
             if t % 2 == 1:
                 image2_stats(1, t // 2)
@@ -393,13 +393,13 @@ def tile_spatialcgnl_pb_kernel(tc, y, Wz, gamma, beta, x, out):
         scalar_row_1(1)
         for t in range(T):
             row_products(1, t)
-            if by_scalar(t):
+            if by_scalar(1, t):
                 scalar_gpsimd_tile(1, t)
                 if t + 3 < T:
                     x_plus_b(1, 2, t + 3, True)
             if t + 2 < T:
                 scalar_row_1(t + 2)
-            for b in range(2 if by_scalar(t) else B):
+            for b in range(2 if by_scalar(1, t) else B):
                 vector_tile(1, b, t)
             for (t0, t1) in STORES_1:
                 if t == t1 - 1:

@@ -24,9 +24,11 @@ N_ST = N_SC + 2 * T
 
 EARLY_ROWS = 4
 LATE_BANKS = 3
+EARLY_BLOCKS = ((0, 2), (2, 4))
+LATE_BLOCKS = ((4, 6), (6, 8))
+BLOCKS_1 = ((0, 2), (2, 4), (4, 6), (6, 8))
+PSUM_Z_BANKS = 6
 CHAIN_AT = (1, 6, 8, 10)
-ROWS_AHEAD = 3
-STORES_1 = ((0, 2), (2, 4), (4, 6), (6, 7), (7, 8))
 
 
 def by_scalar(j, t):
@@ -38,7 +40,7 @@ def tile_spatialcgnl_pb_kernel(tc, y, Wz, gamma, beta, x, out):
     with ExitStack() as ctx:
         keep = ctx.enter_context(tc.tile_pool(name="keep", bufs=1))
         junkp = ctx.enter_context(tc.tile_pool(name="junkp", bufs=2))
-        psum_z = ctx.enter_context(tc.psum_pool(name="psum_z", bufs=6))
+        psum_z = ctx.enter_context(tc.psum_pool(name="psum_z", bufs=PSUM_Z_BANKS))
         psum_a = ctx.enter_context(tc.psum_pool(name="psum_a", bufs=1))
         psum_s = ctx.enter_context(tc.psum_pool(name="psum_s", bufs=1))
 
@@ -215,10 +217,6 @@ def tile_spatialcgnl_pb_kernel(tc, y, Wz, gamma, beta, x, out):
                 nc.vector.tensor_tensor(out=a_sc[j][:], in0=gam_b,
                                         in1=rstd[j][:].unsqueeze(2).to_broadcast([P, B, T]), op=ALU.mult)
 
-        def row_products(j, t):
-            bank[("A", j, t)] = product(j, t, 0)
-            bank[("B", j, t)] = product(j, t, 1)
-
         def z_of(j, b, t):
             if b < 2:
                 return bank[("A", j, t)][:, b * HW:(b + 1) * HW]
@@ -238,11 +236,16 @@ def tile_spatialcgnl_pb_kernel(tc, y, Wz, gamma, beta, x, out):
                                            scalar=a_sc[j][:, b, t:t + 1], in1=xb[b][j][:, cols(t, t + 1)],
                                            op0=ALU.mult, op1=ALU.add)
 
-        def scalar_gpsimd_tile(j, t):
+        def scalar_tile(j, t):
             nc.scalar.activation(out=xb[2][j][:, cols(t, t + 1)], in_=z_of(j, 2, t), func=ACT.Identity,
                                  bias=b_sc[j][:, 2, t:t + 1], scale=a_sc[j][:, 2, t:t + 1])
-            nc.gpsimd.tensor_tensor(out=xb[2][j][:, cols(t, t + 1)], in0=xb[2][j][:, cols(t, t + 1)],
-                                    in1=x_sb[2][j][:, cols(t, t + 1)], op=ALU.add)
+
+        def gpsimd_add(j, rows):
+            if len(rows) > 0:
+                assert rows[-1] + 1 - rows[0] == len(rows)
+                nc.gpsimd.tensor_tensor(out=xb[2][j][:, cols(rows[0], rows[-1] + 1)],
+                                        in0=xb[2][j][:, cols(rows[0], rows[-1] + 1)],
+                                        in1=x_sb[2][j][:, cols(rows[0], rows[-1] + 1)], op=ALU.add)
 
         make_identity(nc, ident[:])
         nc.gpsimd.memset(c_all[:], 1.0 / (CO * HW))
@@ -323,85 +326,102 @@ def tile_spatialcgnl_pb_kernel(tc, y, Wz, gamma, beta, x, out):
         chain(0, 2)
         quantize_w(1, 3)
 
-        scalar_tiles = [(b, t) for t in range(T) for b in range(2)]
-        scalar_done = [0]
+        blocks = (EARLY_BLOCKS + LATE_BLOCKS, BLOCKS_1)
+        scalar_tiles = [[(b, t) for (t0, t1) in blocks[j] for b in range(2) for t in range(t0, t1)] for j in range(G)]
+        scalar_done = [0, 0]
 
-        def scalar_x_plus_b(n):
+        def scalar_x_plus_b(j, n):
             for i in range(n):
-                if scalar_done[0] < len(scalar_tiles):
-                    (b, t) = scalar_tiles[scalar_done[0]]
-                    scalar_done[0] += 1
-                    x_plus_b(0, b, t, False)
+                if scalar_done[j] < len(scalar_tiles[j]):
+                    (b, t) = scalar_tiles[j][scalar_done[j]]
+                    scalar_done[j] += 1
+                    x_plus_b(j, b, t, False)
 
-        rows_written = [0]
+        queue = []
+        issued = [0]
+        free_banks = [PSUM_Z_BANKS]
 
-        def products_up_to(n):
-            while rows_written[0] < min(n, T):
-                row_products(0, rows_written[0])
-                rows_written[0] += 1
+        def enqueue(j, t0, t1):
+            queue.extend([(j, "B", t) for t in range(t0, t1) if by_scalar(j, t)])
+            queue.extend([(j, "A", t) for t in range(t0, t1)])
+            queue.extend([(j, "B", t) for t in range(t0, t1) if not by_scalar(j, t)])
 
-        stores_0 = [(r, r + 1) for r in range(EARLY_ROWS)] + [(r, r + 2) for r in range(EARLY_ROWS, T, 2)]
+        def issue_products():
+            while free_banks[0] > 0 and issued[0] < len(queue):
+                (j, kind, t) = queue[issued[0]]
+                issued[0] += 1
+                bank[(kind, j, t)] = product(j, t, 0 if kind == "A" else 1)
+                free_banks[0] -= 1
+
+        def bank_read():
+            free_banks[0] += 1
+            issue_products()
+
         tiles_done = [0]
 
-        def row_0(t, with_chain):
-            if by_scalar(0, t):
-                scalar_gpsimd_tile(0, t)
-            for b in range(2 if by_scalar(0, t) else B):
-                if with_chain:
-                    for k in range(len(CHAIN_AT)):
-                        if CHAIN_AT[k] == tiles_done[0]:
-                            chain(1, k)
-                    tiles_done[0] += 1
-                vector_tile(0, b, t)
-            for (t0, t1) in stores_0:
-                if t == t1 - 1:
-                    for b in range(B):
-                        store(0, b, t0, t1)
+        def chain_1_step(with_chain):
+            if with_chain:
+                for k in range(len(CHAIN_AT)):
+                    if CHAIN_AT[k] == tiles_done[0]:
+                        chain(1, k)
+                tiles_done[0] += 1
+
+        def gpsimd_x_plus_b(j, t0, t1):
+            for t in range(t0, t1):
+                if not by_scalar(j, t):
+                    x_plus_b(j, 2, t, True)
+
+        def block(j, k, with_chain):
+            (t0, t1) = blocks[j][k]
+            for t in range(t0, t1):
+                if by_scalar(j, t):
+                    scalar_tile(j, t)
+                    bank_read()
+            gpsimd_add(j, [t for t in range(t0, t1) if by_scalar(j, t)])
+            if j == 1 and k + 1 < len(blocks[j]):
+                gpsimd_x_plus_b(j, blocks[j][k + 1][0], blocks[j][k + 1][1])
+            scalar_x_plus_b(j, 2 * (t1 - t0))
+            for b in range(2):
+                for t in range(t0, t1):
+                    chain_1_step(with_chain)
+                    vector_tile(j, b, t)
+                    if b == 1:
+                        bank_read()
+                store(j, b, t0, t1)
+            for t in range(t0, t1):
+                if not by_scalar(j, t):
+                    chain_1_step(with_chain)
+                    vector_tile(j, 2, t)
+                    bank_read()
+            store(j, 2, t0, t1)
 
         def bank_1(t):
             pair_stats(1, t)
             if t == 0:
                 chain(0, 3)
-                for tt in range(T):
-                    if not by_scalar(0, tt):
-                        x_plus_b(0, 2, tt, True)
+                gpsimd_x_plus_b(0, 0, T)
             if t % 2 == 1:
                 image2_stats(1, t // 2)
             if t > 0:
-                scalar_x_plus_b(1)
+                scalar_x_plus_b(0, 1)
 
         for t in range(T - LATE_BANKS):
             bank_1(t)
-        for t in range(EARLY_ROWS):
-            products_up_to(t + 1)
-            row_0(t, False)
-            scalar_x_plus_b(2)
+        for (t0, t1) in EARLY_BLOCKS:
+            enqueue(0, t0, t1)
+        issue_products()
+        for k in range(len(EARLY_BLOCKS)):
+            block(0, k, False)
         for t in range(T - LATE_BANKS, T):
             bank_1(t)
-        products_up_to(EARLY_ROWS + ROWS_AHEAD)
-        for t in range(EARLY_ROWS, T):
-            row_0(t, True)
-            products_up_to(t + ROWS_AHEAD)
-            scalar_x_plus_b(2)
+        for j in range(G):
+            for (t0, t1) in (LATE_BLOCKS, BLOCKS_1)[j]:
+                enqueue(j, t0, t1)
+        issue_products()
+        for k in range(len(EARLY_BLOCKS), len(blocks[0])):
+            block(0, k, True)
 
-        def scalar_row_1(t):
-            x_plus_b(1, 0, t, False)
-            x_plus_b(1, 1, t, False)
-
-        x_plus_b(1, 2, 1, True)
-        scalar_row_1(0)
-        scalar_row_1(1)
-        for t in range(T):
-            row_products(1, t)
-            if by_scalar(1, t):
-                scalar_gpsimd_tile(1, t)
-                if t + 3 < T:
-                    x_plus_b(1, 2, t + 3, True)
-            if t + 2 < T:
-                scalar_row_1(t + 2)
-            for b in range(2 if by_scalar(1, t) else B):
-                vector_tile(1, b, t)
-            for (t0, t1) in STORES_1:
-                if t == t1 - 1:
-                    for b in range(B):
-                        store(1, b, t0, t1)
+        gpsimd_x_plus_b(1, BLOCKS_1[0][0], BLOCKS_1[0][1])
+        scalar_x_plus_b(1, 2 * (BLOCKS_1[0][1] - BLOCKS_1[0][0]))
+        for k in range(len(BLOCKS_1)):
+            block(1, k, False)

@@ -28,7 +28,7 @@ EARLY_BLOCKS = ((0, 2), (2, 4))
 LATE_BLOCKS = ((4, 6), (6, 8))
 BLOCKS_1 = ((0, 2), (2, 4), (4, 6), (6, 8))
 PSUM_Z_BANKS = 6
-CHAIN_AT = (1, 6, 8, 10)
+CHAIN_AT = (2, 5, 7, 9)
 
 
 def by_scalar(j, t):
@@ -314,10 +314,9 @@ def tile_spatialcgnl_pb_kernel(tc, y, Wz, gamma, beta, x, out):
             transpose_w(1, s)
         for s in range(4):
             copy_w(1, s)
-        quantize_y(1, 0, 1)
-        chain(0, 0)
         interleave_y(1, 2, False)
-        quantize_y(1, 1, 2)
+        chain(0, 0)
+        quantize_y(1, 0, 2)
         quantize_y(1, 2, 3)
         quantize_w(1, 0)
         quantize_w(1, 1)
@@ -380,7 +379,12 @@ def tile_spatialcgnl_pb_kernel(tc, y, Wz, gamma, beta, x, out):
             gpsimd_add(j, [t for t in range(t0, t1) if by_scalar(j, t)])
             if j == 1 and k + 1 < len(blocks[j]):
                 gpsimd_x_plus_b(j, blocks[j][k + 1][0], blocks[j][k + 1][1])
-            scalar_x_plus_b(j, 2 * (t1 - t0))
+            ahead = 2 * (t1 - t0)
+            if j == 0 and k == len(EARLY_BLOCKS) - 1:
+                ahead = t1 - t0
+            if j == 0 and k == len(EARLY_BLOCKS):
+                ahead = 3 * (t1 - t0)
+            scalar_x_plus_b(j, ahead)
             for b in range(2):
                 for t in range(t0, t1):
                     chain_1_step(with_chain)
@@ -402,7 +406,7 @@ def tile_spatialcgnl_pb_kernel(tc, y, Wz, gamma, beta, x, out):
                 gpsimd_x_plus_b(0, 0, T)
             if t % 2 == 1:
                 image2_stats(1, t // 2)
-            if t > 0:
+            if 0 < t < T - LATE_BANKS:
                 scalar_x_plus_b(0, 1)
 
         for t in range(T - LATE_BANKS):

@@ -26,13 +26,13 @@ EARLY_ROWS = 4
 LATE_BANKS = 3
 EARLY_BLOCKS = ((0, 2), (2, 4))
 LATE_BLOCKS = ((4, 6), (6, 8))
-BLOCKS_1 = ((0, 2), (2, 4), (4, 6), (6, 8))
+BLOCKS_1 = ((0, 2), (2, 5), (5, 8))
 PSUM_Z_BANKS = 6
 CHAIN_AT = (2, 5, 7, 9)
 
 
 def by_scalar(j, t):
-    return t < EARLY_ROWS if j == 0 else t % 2 == 0
+    return t < EARLY_ROWS if j == 0 else t + 1 not in [t1 for (t0, t1) in BLOCKS_1]
 
 
 def tile_spatialcgnl_pb_kernel(tc, y, Wz, gamma, beta, x, out):

from contextlib import ExitStack

import concourse.mybir as mybir
from concourse.masks import make_identity

F32 = mybir.dt.float32
BF16 = mybir.dt.bfloat16
U32 = mybir.dt.uint32
U8 = mybir.dt.uint8
E5X4 = mybir.dt.float8_e5m2_x4
ACT = mybir.ActivationFunctionType
ALU = mybir.AluOpType
AX = mybir.AxisListType

B, G, CG, CO, HW = 3, 2, 512, 1024, 256
P = 128
T = CO // P
EPS = 1e-5
FLOPS = 2 * B * G * CO * CG * HW

N_BN = 6 * T
N_SC = N_BN + 8
N_ST = N_SC + 2 * T

EARLY_ROWS = 4
LATE_BANKS = 3
EARLY_BLOCKS = ((0, 2), (2, 4))
LATE_BLOCKS = ((4, 6), (6, 8))
BLOCKS_1 = ((0, 2), (2, 5), (5, 8))
PSUM_Z_BANKS = 6
CHAIN_AT = (2, 5, 7, 9)


def by_scalar(j, t):
    return t < EARLY_ROWS if j == 0 else t + 1 not in [t1 for (t0, t1) in BLOCKS_1]


def tile_spatialcgnl_pb_kernel(tc, y, Wz, gamma, beta, x, out):
    nc = tc.nc
    with ExitStack() as ctx:
        keep = ctx.enter_context(tc.tile_pool(name="keep", bufs=1))
        junkp = ctx.enter_context(tc.tile_pool(name="junkp", bufs=2))
        psum_z = ctx.enter_context(tc.psum_pool(name="psum_z", bufs=PSUM_Z_BANKS))
        psum_a = ctx.enter_context(tc.psum_pool(name="psum_a", bufs=1))
        psum_s = ctx.enter_context(tc.psum_pool(name="psum_s", bufs=1))

        ident = keep.tile([P, P], F32, name="ident")
        c_all = keep.tile([P, P], F32, name="c_all")
        one = keep.tile([P, 1], F32, name="one")
        warm = keep.tile([P, 1], F32, name="warm")
        y_raw = [keep.tile([P, B, 4 * HW], BF16, name="y_raw%d" % j) for j in range(G)]
        w_raw = [keep.tile([P, T, CG], BF16, name="w_raw%d" % j) for j in range(G)]
        x_sb = [[keep.tile([P, T * HW], BF16, name="x_sb%d_%d" % (b, j)) for j in range(G)] for b in range(B)]
        gam = keep.tile([P, G, T], BF16, name="gam")
        bet = keep.tile([P, G, T], BF16, name="bet")
        y_grp = [keep.tile([P, B, 4 * HW], BF16, name="y_grp0", align_bytes=64), None]
        y_cod = [keep.tile([P, B * HW], U32, name="y_cod%d" % j, align_bytes=64) for j in range(G)]
        y_scl = [keep.tile([P, B * HW], U8, name="y_scl%d" % j, align_bytes=64) for j in range(G)]
        w_grp = [keep.tile([P, T * CG], BF16, name="w_grp0", tag="shared", align_bytes=64),
                 keep.tile([P, T * CG], BF16, name="w_grp1", align_bytes=64)]
        w_cod = [keep.tile([P, CO], U32, name="w_cod%d" % j, align_bytes=64) for j in range(G)]
        w_scl = [keep.tile([P, CO], U8, name="w_scl%d" % j, align_bytes=64) for j in range(G)]
        st = [keep.tile([P, N_ST], F32, name="st%d" % j) for j in range(G)]
        gmn = [keep.tile([P, B, T], F32, name="gmn%d" % j) for j in range(G)]
        a_sc = [keep.tile([P, B, T], F32, name="a_sc%d" % j) for j in range(G)]
        b_sc = [keep.tile([P, B, T], F32, name="b_sc%d" % j) for j in range(G)]
        xb = [[keep.tile([P, T * HW], F32, name="xb%d_%d" % (b, j)) for j in range(G)] for b in range(B)]
        tot = [keep.tile([P, B, 2], F32, name="tot%d" % j) for j in range(G)]
        nvar = [keep.tile([P, B], F32, name="nvar%d" % j) for j in range(G)]
        rstd = [keep.tile([P, B], F32, name="rstd%d" % j) for j in range(G)]
        bank = {}

        def chan_view(ap, b, j):
            return ap[b].rearrange("(j p t) h w -> j p (t h w)", j=G, t=T)[j]

        def cols(t0, t1):
            return slice(t0 * HW, t1 * HW)

        def load_y(j, b0, b1):
            nc.sync.dma_start(out=y_raw[j][:, b0:b1, :], in_=y[b0:b1, j].rearrange("b (p q) w -> p b (q w)", q=4))

        def load_w(j, t0, t1):
            nc.sync.dma_start(out=w_raw[j][:, t0:t1, :], in_=Wz[j].rearrange("(p t) k -> p t k", t=T)[:, t0:t1, :])

        def store(j, b, t0, t1):
            nc.sync.dma_start(out=chan_view(out, b, j)[:, cols(t0, t1)], in_=xb[b][j][:, cols(t0, t1)])

        def interleave_y(j, b, on_gpsimd):
            if on_gpsimd:
                nc.gpsimd.tensor_scalar(
                    out=y_grp[j][:, b, :].rearrange("p (w q) -> p w q", q=4),
                    in0=y_raw[j][:, b, :].rearrange("p (q w) -> p w q", q=4),
                    scalar1=1.0, scalar2=0.0, op0=ALU.mult, op1=ALU.add,
                )
            else:
                nc.vector.tensor_copy(
                    out=y_grp[j][:, b:b + 1, :].rearrange("p b (w q) -> p b w q", q=4),
                    in_=y_raw[j][:, b:b + 1, :].rearrange("p b (q w) -> p b w q", q=4),
                )

        def quantize_y(j, b0, b1):
            nc.vector.quantize_mx(
                out=y_cod[j][:, b0 * HW:b1 * HW].bitcast(E5X4),
                scales=y_scl[j][:, b0 * HW:b1 * HW],
                in_=y_grp[j][:, b0:b1, :].rearrange("p b c -> p (b c)"),
            )

        def transpose_w(j, s):
            words = w_raw[j][:].bitcast(F32)
            z = psum_z.tile([P, 512], F32, name="z")
            bank[("t", j, s)] = z
            tp = z[:].rearrange("p (s u r) -> p s u r", s=2, u=2)
            for tt in range(2):
                for u in range(2):
                    nc.tensor.transpose(tp[:, tt, u, :], words[:, 2 * s + tt, u:CG // 2:2], ident[:])

        def copy_w(j, s):
            gwords = w_grp[j][:].bitcast(F32)
            nc.scalar.copy(
                out=gwords[:, 512 * s:512 * (s + 1)].rearrange("p (s r u) -> p s r u", s=2, u=2),
                in_=bank[("t", j, s)][:].rearrange("p (s u r) -> p s r u", s=2, u=2),
            )

        def quantize_w(j, s):
            nc.vector.quantize_mx(
                out=w_cod[j][:, 256 * s:256 * (s + 1)].bitcast(E5X4),
                scales=w_scl[j][:, 256 * s:256 * (s + 1)],
                in_=w_grp[j][:, 1024 * s:1024 * (s + 1)],
            )

        def product(j, t, first_image):
            c0 = first_image * HW
            z = psum_z.tile([P, 512], F32, name="z")
            nc.tensor.matmul_mx(
                out=z[:],
                lhsT=w_cod[j][:, P * t:P * (t + 1)].bitcast(E5X4),
                lhsT_scale=w_scl[j][:, P * t:P * (t + 1)],
                rhs=y_cod[j][:, c0:c0 + 512].bitcast(E5X4),
                rhs_scale=y_scl[j][:, c0:c0 + 512],
                start=True,
                stop=True,
            )
            return z

        def position_pass(z, j, m, h, start, stop):
            c0 = 2 * HW + P * m
            nc.tensor.matmul_mx(
                out=z[:],
                lhsT=y_cod[j][:, c0:c0 + P].bitcast(E5X4),
                lhsT_scale=y_scl[j][:, c0:c0 + P],
                rhs=w_cod[j][:, 512 * h:512 * (h + 1)].bitcast(E5X4),
                rhs_scale=w_scl[j][:, 512 * h:512 * (h + 1)],
                start=start,
                stop=stop,
            )

        def pair_product(j, t):
            bank[("X", j, t)] = product(j, t, 0)

        def pair_bn(j, t):
            nc.vector.bn_stats(out=st[j][:, 6 * t:6 * t + 6],
                               in_=bank[("X", j, t)][:].rearrange("p (i n) -> p n i", i=2))

        def pair_stats(j, t):
            pair_product(j, t)
            pair_bn(j, t)

        def image2_stats(j, k):
            (h, m) = (k // 2, k % 2)
            z = psum_z.tile([P, 512], F32, name="z")
            position_pass(z, j, m, h, True, True)
            if k == 0:
                bank[("a", j)] = psum_a.tile([P, 512], F32, name="za")
            position_pass(bank[("a", j)], j, m, h, k == 0, k == 3)
            jk = junkp.tile([P, 512], BF16, name="jk")
            nc.scalar.activation(out=jk[:], in_=z[:], func=ACT.Square, accum_out=st[j][:, N_BN + 4 + k:N_BN + 5 + k])
            if k == 3:
                jk = junkp.tile([P, 512], BF16, name="jk")
                nc.scalar.activation(out=jk[:], in_=bank[("a", j)][:], func=ACT.Identity,
                                     accum_out=st[j][:, N_BN:N_BN + 1])

        def bn_view(ap):
            return ap[:, 0:N_BN].rearrange("p (t i k) -> p i t k", i=2, k=3)

        def chain(j, step):
            gam_b = gam[:, j:j + 1, :].to_broadcast([P, B, T])
            if step == 0:
                v = bn_view(st[j])
                nc.vector.scalar_tensor_tensor(out=v[:, :, :, 0], in0=v[:, :, :, 1], scalar=float(HW),
                                               in1=v[:, :, :, 1], op0=ALU.mult, op1=ALU.mult)
                nc.vector.tensor_scalar(out=st[j][:, N_SC:N_ST].rearrange("p (t i) -> p i t", i=2), in0=v[:, :, :, 1],
                                        scalar1=float(HW), scalar2=0.0, op0=ALU.mult, op1=ALU.add)
                ps = psum_s.tile([P, N_ST], F32, name="ps")
                bank[("c", j)] = ps
                nc.tensor.matmul(ps[:], lhsT=c_all[:], rhs=st[j][:], start=True, stop=True)
            elif step == 1:
                ps = bank[("c", j)]
                nc.vector.tensor_reduce(out=tot[j][:, 0:2, 1], in_=bn_view(ps)[:, :, :, 0:3:2], axis=AX.XY, op=ALU.add)
                nc.vector.tensor_reduce(out=tot[j][:, 0:2, 0], in_=ps[:, N_SC:N_ST].rearrange("p (t i) -> p i t", i=2),
                                        axis=AX.X, op=ALU.add)
                nc.vector.tensor_reduce(out=tot[j][:, 2, :], in_=ps[:, N_BN:N_SC].rearrange("p (k f) -> p k f", f=4),
                                        axis=AX.X, op=ALU.add)
            elif step == 2:
                for b in range(B):
                    nc.vector.scalar_tensor_tensor(out=nvar[j][:, b:b + 1], in0=tot[j][:, b, 0:1],
                                                   scalar=tot[j][:, b, 0:1], in1=tot[j][:, b, 1:2],
                                                   op0=ALU.mult, op1=ALU.subtract)
                nc.vector.scalar_tensor_tensor(out=gmn[j][:], in0=gam_b, scalar=-1.0,
                                               in1=tot[j][:, :, 0].unsqueeze(2).to_broadcast([P, B, T]),
                                               op0=ALU.mult, op1=ALU.mult)
                nc.scalar.activation(out=rstd[j][:], in_=nvar[j][:], func=ACT.Abs_reciprocal_sqrt, bias=EPS, scale=-1.0)
            else:
                for b in range(B):
                    nc.vector.scalar_tensor_tensor(out=b_sc[j][:, b, :], in0=gmn[j][:, b, :],
                                                   scalar=rstd[j][:, b:b + 1], in1=bet[:, j, :],
                                                   op0=ALU.mult, op1=ALU.add)
                nc.vector.tensor_tensor(out=a_sc[j][:], in0=gam_b,
                                        in1=rstd[j][:].unsqueeze(2).to_broadcast([P, B, T]), op=ALU.mult)

        def z_of(j, b, t):
            if b < 2:
                return bank[("A", j, t)][:, b * HW:(b + 1) * HW]
            return bank[("B", j, t)][:, HW:2 * HW]

        def x_plus_b(j, b, t, on_gpsimd):
            if on_gpsimd:
                nc.gpsimd.tensor_scalar(out=xb[b][j][:, cols(t, t + 1)], in0=x_sb[b][j][:, cols(t, t + 1)],
                                        scalar1=one[:, 0:1], scalar2=b_sc[j][:, b, t:t + 1],
                                        op0=ALU.mult, op1=ALU.add)
            else:
                nc.scalar.activation(out=xb[b][j][:, cols(t, t + 1)], in_=x_sb[b][j][:, cols(t, t + 1)],
                                     func=ACT.Identity, bias=b_sc[j][:, b, t:t + 1], scale=1.0)

        def vector_tile(j, b, t):
            nc.vector.scalar_tensor_tensor(out=xb[b][j][:, cols(t, t + 1)], in0=z_of(j, b, t),
                                           scalar=a_sc[j][:, b, t:t + 1], in1=xb[b][j][:, cols(t, t + 1)],
                                           op0=ALU.mult, op1=ALU.add)

        def scalar_tile(j, t):
            nc.scalar.activation(out=xb[2][j][:, cols(t, t + 1)], in_=z_of(j, 2, t), func=ACT.Identity,
                                 bias=b_sc[j][:, 2, t:t + 1], scale=a_sc[j][:, 2, t:t + 1])

        def gpsimd_add(j, rows):
            if len(rows) > 0:
                assert rows[-1] + 1 - rows[0] == len(rows)
                nc.gpsimd.tensor_tensor(out=xb[2][j][:, cols(rows[0], rows[-1] + 1)],
                                        in0=xb[2][j][:, cols(rows[0], rows[-1] + 1)],
                                        in1=x_sb[2][j][:, cols(rows[0], rows[-1] + 1)], op=ALU.add)

        make_identity(nc, ident[:])
        nc.gpsimd.memset(c_all[:], 1.0 / (CO * HW))
        nc.vector.memset(one[:], 1.0)
        nc.scalar.activation(out=warm[:], in_=one[:], func=ACT.Abs_reciprocal_sqrt)
        for j in range(G):
            nc.gpsimd.memset(st[j][:, N_BN:N_SC], 0.0)

        ctx.enter_context(tc.manual_schedule())

        load_y(0, 0, 1)
        load_y(0, 1, 2)
        load_w(0, 0, 2)
        load_y(0, 2, 3)
        load_w(0, 2, 4)
        load_w(0, 4, 6)
        load_w(0, 6, 8)
        load_y(1, 0, 3)
        load_w(1, 0, 4)
        load_w(1, 4, 8)
        nc.sync.dma_start(out=gam[:], in_=gamma.rearrange("(j p t) -> p j t", j=G, t=T))
        nc.sync.dma_start(out=bet[:], in_=beta.rearrange("(j p t) -> p j t", j=G, t=T))
        for j in range(G):
            for b in range(B):
                nc.sync.dma_start(out=x_sb[b][j][:], in_=chan_view(x, b, j))

        interleave_y(0, 0, False)
        interleave_y(0, 1, False)
        quantize_y(0, 0, 1)
        quantize_y(0, 1, 2)
        transpose_w(0, 0)
        copy_w(0, 0)
        transpose_w(0, 1)
        copy_w(0, 1)
        transpose_w(0, 2)
        copy_w(0, 2)
        interleave_y(0, 2, False)
        quantize_w(0, 0)
        quantize_y(0, 2, 3)
        quantize_w(0, 1)
        pair_product(0, 0)
        pair_product(0, 1)
        transpose_w(0, 3)
        copy_w(0, 3)
        pair_product(0, 2)
        pair_product(0, 3)
        pair_bn(0, 0)
        quantize_w(0, 2)
        pair_bn(0, 1)
        quantize_w(0, 3)
        y_grp[1] = keep.tile([P, B, 4 * HW], BF16, name="y_grp1", tag="shared", align_bytes=64)
        interleave_y(1, 0, True)
        interleave_y(1, 1, True)
        pair_bn(0, 2)
        pair_bn(0, 3)
        image2_stats(0, 0)
        image2_stats(0, 1)
        pair_stats(0, 4)
        pair_stats(0, 5)
        image2_stats(0, 2)
        pair_stats(0, 6)
        pair_stats(0, 7)
        image2_stats(0, 3)

        for s in range(4):
            transpose_w(1, s)
        for s in range(4):
            copy_w(1, s)
        interleave_y(1, 2, False)
        chain(0, 0)
        quantize_y(1, 0, 2)
        quantize_y(1, 2, 3)
        quantize_w(1, 0)
        quantize_w(1, 1)
        chain(0, 1)
        quantize_w(1, 2)
        chain(0, 2)
        quantize_w(1, 3)

        blocks = (EARLY_BLOCKS + LATE_BLOCKS, BLOCKS_1)
        scalar_tiles = [[(b, t) for (t0, t1) in blocks[j] for b in range(2) for t in range(t0, t1)] for j in range(G)]
        scalar_done = [0, 0]

        def scalar_x_plus_b(j, n):
            for i in range(n):
                if scalar_done[j] < len(scalar_tiles[j]):
                    (b, t) = scalar_tiles[j][scalar_done[j]]
                    scalar_done[j] += 1
                    x_plus_b(j, b, t, False)

        queue = []
        issued = [0]
        free_banks = [PSUM_Z_BANKS]

        def enqueue(j, t0, t1):
            queue.extend([(j, "B", t) for t in range(t0, t1) if by_scalar(j, t)])
            queue.extend([(j, "A", t) for t in range(t0, t1)])
            queue.extend([(j, "B", t) for t in range(t0, t1) if not by_scalar(j, t)])

        def issue_products():
            while free_banks[0] > 0 and issued[0] < len(queue):
                (j, kind, t) = queue[issued[0]]
                issued[0] += 1
                bank[(kind, j, t)] = product(j, t, 0 if kind == "A" else 1)
                free_banks[0] -= 1

        def bank_read():
            free_banks[0] += 1
            issue_products()

        tiles_done = [0]

        def chain_1_step(with_chain):
            if with_chain:
                for k in range(len(CHAIN_AT)):
                    if CHAIN_AT[k] == tiles_done[0]:
                        chain(1, k)
                tiles_done[0] += 1

        def gpsimd_x_plus_b(j, t0, t1):
            for t in range(t0, t1):
                if not by_scalar(j, t):
                    x_plus_b(j, 2, t, True)

        def block(j, k, with_chain):
            (t0, t1) = blocks[j][k]
            for t in range(t0, t1):
                if by_scalar(j, t):
                    scalar_tile(j, t)
                    bank_read()
            gpsimd_add(j, [t for t in range(t0, t1) if by_scalar(j, t)])
            if j == 1 and k + 1 < len(blocks[j]):
                gpsimd_x_plus_b(j, blocks[j][k + 1][0], blocks[j][k + 1][1])
            ahead = 2 * (t1 - t0)
            if j == 0 and k == len(EARLY_BLOCKS) - 1:
                ahead = t1 - t0
            if j == 0 and k == len(EARLY_BLOCKS):
                ahead = 3 * (t1 - t0)
            scalar_x_plus_b(j, ahead)
            for b in range(2):
                for t in range(t0, t1):
                    chain_1_step(with_chain)
                    vector_tile(j, b, t)
                    if b == 1:
                        bank_read()
                store(j, b, t0, t1)
            for t in range(t0, t1):
                if not by_scalar(j, t):
                    chain_1_step(with_chain)
                    vector_tile(j, 2, t)
                    bank_read()
            store(j, 2, t0, t1)

        def bank_1(t):
            pair_stats(1, t)
            if t == 0:
                chain(0, 3)
                gpsimd_x_plus_b(0, 0, T)
            if t % 2 == 1:
                image2_stats(1, t // 2)
            if 0 < t < T - LATE_BANKS:
                scalar_x_plus_b(0, 1)

        for t in range(T - LATE_BANKS):
            bank_1(t)
        for (t0, t1) in EARLY_BLOCKS:
            enqueue(0, t0, t1)
        issue_products()
        for k in range(len(EARLY_BLOCKS)):
            block(0, k, False)
        for t in range(T - LATE_BANKS, T):
            bank_1(t)
        for j in range(G):
            for (t0, t1) in (LATE_BLOCKS, BLOCKS_1)[j]:
                enqueue(j, t0, t1)
        issue_products()
        for k in range(len(EARLY_BLOCKS), len(blocks[0])):
            block(0, k, True)

        gpsimd_x_plus_b(1, BLOCKS_1[0][0], BLOCKS_1[0][1])
        scalar_x_plus_b(1, 2 * (BLOCKS_1[0][1] - BLOCKS_1[0][0]))
        for k in range(len(BLOCKS_1)):
            block(1, k, False)
